import numpy as np
import ml_dtypes


def mxq(x, axis, fmt="e4m3"):
    dtype, down = {"e4m3": (ml_dtypes.float8_e4m3fn, 7), "e5m2": (ml_dtypes.float8_e5m2, 14)}[fmt]
    v = np.moveaxis(np.asarray(x, np.float32).astype(ml_dtypes.bfloat16).astype(np.float64), axis, -1)
    blocks = v.reshape(v.shape[:-1] + (-1, 32))
    amax = np.abs(blocks).max(-1, keepdims=True)
    byte = np.maximum(np.where(amax > 0, np.frexp(amax)[1] - 1 + 127, 0) - down, 1)
    scale = np.exp2(byte - 127.0)
    codes = (blocks / scale).astype(np.float32).astype(dtype).astype(np.float64)
    return np.moveaxis((codes * scale).reshape(v.shape), -1, axis)


WIDE = False


def mx_kscale(k):
    if not WIDE:
        return np.ones(k)
    levels = np.array([10, -10, 5, -5, 0])
    if k % 512:
        return np.exp2(np.random.permutation(np.resize(levels, k // 32))).repeat(32)
    a = np.empty((k // 512, 16))
    for p in range(k // 512):
        a[p, :8] = np.random.permutation(np.resize(levels, 8))
        for g in range(8):
            far = levels[np.abs(levels - a[p, g]) >= 10]
            a[p, g + 8] = far[np.random.randint(len(far))]
    return np.exp2(a.ravel()).repeat(32)


BF16 = ml_dtypes.bfloat16


def bf(x):
    return np.asarray(x, np.float32).astype(BF16)


def f64(x):
    return np.asarray(x).astype(np.float64)


B, T, D, O = 16, 32, 16384, 512


def erf(z):
    a = np.clip(z, -6.0, 6.0)
    q = 2.0 * a * a
    term = a.copy()
    total = a.copy()
    for k in range(1, 130):
        term = term * q / (2 * k + 1)
        total = total + term
    return 2.0 / np.sqrt(np.pi) * np.exp(-a * a) * total


def gelu_exact(v):
    return 0.5 * v * (1.0 + erf(v / np.sqrt(2.0)))


def setup_inputs():
    s = mx_kscale(D)
    x = np.random.standard_normal((B, T, D)) * s
    lengths = np.random.randint(T // 4, T + 1, size=B)
    lengths[np.random.randint(B)] = T
    pad = np.arange(T)[None, :] >= lengths[:, None]
    x = np.where(pad[:, :, None], -1.0, x)
    return {"x": bf(x), "W": bf(np.random.standard_normal((O, D)) / np.sqrt(D) / s[None, :]), "b": bf(np.random.standard_normal(O) * 0.3)}


def reference(x, W, b):
    x = f64(x)
    valid = ~np.all(x == -1.0, axis=-1)
    y = gelu_exact((mxq(x, 2, "e4m3") @ mxq(f64(W), 1, "e4m3").T) + f64(b))
    vf = valid[..., None].astype(np.float64)
    n = np.sum(vf, axis=1)
    mean = np.sum(y * vf, axis=1) / n
    diff = (y - mean[:, None, :]) * vf
    var = np.sum(diff * diff, axis=1) / np.maximum(n - 1.0, 1.0)
    std = np.where(n > 1.0, np.sqrt(var), np.zeros_like(var))
    out = np.concatenate([std, mean], axis=-1)
    return np.where(np.isnan(out), np.zeros_like(out), out)

@@ -1,0 +1,290 @@
+from contextlib import ExitStack
+
+import concourse.mybir as mybir
+from concourse.masks import make_identity
+
+F32 = mybir.dt.float32
+BF16 = mybir.dt.bfloat16
+U32 = mybir.dt.uint32
+U8 = mybir.dt.uint8
+FP8X4 = mybir.dt.float8_e4m3fn_x4
+ALU = mybir.AluOpType
+ACT = mybir.ActivationFunctionType
+AX = mybir.AxisListType
+
+P = 128
+SAMPLES, TOKENS, D, O = 16, 32, 16384, 512
+ROWS = SAMPLES * TOKENS
+ROW_TILES = ROWS // P
+K_PASS = 4 * P
+WORDS_PASS = K_PASS // 2
+ROUNDS = D // K_PASS
+
+CHUNK_MAX = 4 * K_PASS
+CHUNK_WIDTHS = [K_PASS] * 4 + [2 * K_PASS] * 2 + [CHUNK_MAX] * (D // CHUNK_MAX - 2)
+CHUNKS_AHEAD = 3
+
+PASS_LAG = 2
+
+HELD_TILE = ROW_TILES - 1
+HELD = 24
+
+PAD_WORD = -(1.0 + 49024.0 / 8388608.0)
+SQRT_FLOOR = 2.0 ** -100
+
+FLOPS = 2 * ROWS * O * D
+
+
+def tile_linearnnencoder_k_kernel(tc, x, W, b, out):
+    nc = tc.nc
+    assert sum(CHUNK_WIDTHS) == D
+
+    x_rows = x.rearrange("s t k -> (s t) k").rearrange("(a p) k -> p a k", p=P)
+    w_rows = W.rearrange("(a p) k -> p a k", p=P)
+
+    with ExitStack() as ctx:
+        ctx.enter_context(tc.manual_schedule())
+        const = ctx.enter_context(tc.tile_pool(name="const", bufs=1))
+        natural = ctx.enter_context(tc.tile_pool(name="natural", bufs=CHUNKS_AHEAD))
+        grouped = ctx.enter_context(tc.tile_pool(name="grouped", bufs=2))
+        packed = ctx.enter_context(tc.tile_pool(name="packed", bufs=PASS_LAG + 2))
+        packed_held = ctx.enter_context(tc.tile_pool(name="packed_held", bufs=HELD))
+        scratch = ctx.enter_context(tc.tile_pool(name="scratch", bufs=2))
+        tail = ctx.enter_context(tc.tile_pool(name="tail", bufs=2))
+        acc_pool = ctx.enter_context(tc.psum_pool(name="acc", bufs=1))
+        flip_pool = ctx.enter_context(tc.psum_pool(name="flip", bufs=1))
+
+        chunk_start = [sum(CHUNK_WIDTHS[:c]) for c in range(len(CHUNK_WIDTHS))]
+        chunk_tiles = {}
+
+        def load_chunk(c):
+            k0, width = chunk_start[c], CHUNK_WIDTHS[c]
+            x_nat = natural.tile([P, ROW_TILES, CHUNK_MAX], BF16, name="x_nat")
+            nc.sync.dma_start(out=x_nat[:, :, :width], in_=x_rows[:, :, k0 : k0 + width])
+            w_nat = natural.tile([P, ROW_TILES, CHUNK_MAX], BF16, name="w_nat")
+            nc.sync.dma_start(out=w_nat[:, :, :width], in_=w_rows[:, :, k0 : k0 + width])
+            chunk_tiles[c] = (x_nat, w_nat)
+
+        def as_words(nat):
+            flat = nat[:].rearrange("p a k -> p (a k)").bitcast(F32)
+            return flat.rearrange("p (a w) -> p a w", a=ROW_TILES)
+
+        for c in range(CHUNKS_AHEAD):
+            load_chunk(c)
+
+        ident = const.tile([P, P], F32, name="ident")
+        make_identity(nc, ident[:])
+
+        b_rows = const.tile([P, P], BF16, name="b_rows")
+        nc.vector.memset(b_rows[:], 0.0)
+        nc.scalar.dma_start(out=b_rows[0:ROW_TILES, :], in_=b.rearrange("(m o) -> m o", o=P))
+        b_rows32 = const.tile([P, P], F32, name="b_rows32")
+        nc.vector.tensor_copy(out=b_rows32[:], in_=b_rows[:])
+
+        one = const.tile([P, 1], F32, name="one")
+        nc.vector.memset(one[:], 1.0)
+        warm = const.tile([P, 2], F32, name="warm")
+        nc.scalar.activation(out=warm[:, 0:1], in_=one[:], func=ACT.Gelu)
+
+        differing = const.tile([P, ROW_TILES, len(CHUNK_WIDTHS)], F32, name="differing")
+
+        acc = [acc_pool.tile([P, ROWS], F32, name="acc%d" % m) for m in range(ROW_TILES)]
+
+        def flip_rows(words, word0, label):
+            banks = []
+            for half in range(2):
+                bank = flip_pool.tile([P, 2, 2, P], F32, name="%s_flip%d" % (label, half))
+                for i in range(2):
+                    for u in range(2):
+                        nc.tensor.transpose(
+                            bank[:, i, u, :],
+                            words[:, 2 * half + i, word0 + u : word0 + WORDS_PASS : 2],
+                            ident[:],
+                        )
+                banks.append(bank)
+            return banks
+
+        def gather_words(banks, label):
+            rows4 = grouped.tile([P, 4 * ROWS], BF16, name="%s_rows4" % label, align_bytes=64)
+            by_row = rows4[:].bitcast(F32).rearrange("p (a r u) -> p a r u", a=ROW_TILES, u=2)
+            for half in range(2):
+                nc.scalar.copy(
+                    out=by_row[:, 2 * half : 2 * half + 2, :, :],
+                    in_=banks[half][:].rearrange("p i u r -> p i r u"),
+                )
+            return rows4
+
+        def quantise(rows4, n_rows, pool, label):
+            codes = pool.tile([P, n_rows], U32, name="%s_codes" % label, align_bytes=64)
+            scales = pool.tile([P, n_rows], U8, name="%s_scales" % label, align_bytes=64)
+            nc.vector.quantize_mx(out=codes[:].bitcast(FP8X4), scales=scales[:], in_=rows4)
+            return codes, scales
+
+        def multiply(operands, r, m):
+            x_codes, x_scales = operands[0]
+            w_codes, w_scales = operands[1 + m]
+            nc.tensor.matmul_mx(
+                out=acc[m][:],
+                lhsT=w_codes[:].bitcast(FP8X4),
+                lhsT_scale=w_scales[:],
+                rhs=x_codes[:].bitcast(FP8X4),
+                rhs_scale=x_scales[:],
+                start=(r == 0),
+                stop=(r == ROUNDS - 1),
+            )
+
+        def test_padding(words, c, a):
+            n_words = CHUNK_WIDTHS[c] // 2
+            unequal = scratch.tile([P, CHUNK_MAX // 2], BF16, name="unequal")
+            nc.vector.tensor_scalar(
+                out=unequal[:, :n_words],
+                in0=words[:, a, :n_words],
+                scalar1=PAD_WORD,
+                scalar2=None,
+                op0=ALU.not_equal,
+                op1=ALU.add,
+                accum_out=differing[:, a, c : c + 1],
+            )
+
+        def find_valid_tokens():
+            total = const.tile([P, ROW_TILES], F32, name="total")
+            nc.vector.tensor_reduce(out=total[:], in_=differing[:], axis=AX.X, op=ALU.add)
+            valid_col = const.tile([P, ROW_TILES], F32, name="valid_col")
+            nc.vector.tensor_single_scalar(out=valid_col[:], in_=total[:], scalar=0.0, op=ALU.is_gt)
+            return valid_col
+
+        def multiply_round(r):
+            for m in range(ROW_TILES):
+                if m != HELD_TILE or r < ROUNDS - HELD:
+                    multiply(quantised[r], r, m)
+
+        quantised = []
+        r = 0
+        for c in range(len(CHUNK_WIDTHS)):
+            x_words = as_words(chunk_tiles[c][0])
+            w_words = as_words(chunk_tiles[c][1])
+            rounds_here = CHUNK_WIDTHS[c] // K_PASS
+            tests_a_round = ROW_TILES // rounds_here
+            for j in range(rounds_here):
+                x_banks = flip_rows(x_words, WORDS_PASS * j, "x")
+                w_banks = flip_rows(w_words, WORDS_PASS * j, "w")
+                x_rows4 = gather_words(x_banks, "x")
+                w_rows4 = gather_words(w_banks, "w")
+                if r >= PASS_LAG:
+                    multiply_round(r - PASS_LAG)
+                for a in range(tests_a_round * j, tests_a_round * (j + 1)):
+                    test_padding(x_words, c, a)
+                if r == ROUNDS - 1:
+                    valid_col = find_valid_tokens()
+                operands = [quantise(x_rows4[:], ROWS, packed_held, "x")]
+                for m in range(ROW_TILES):
+                    operands.append(
+                        quantise(
+                            w_rows4[:, 4 * P * m : 4 * P * (m + 1)],
+                            P,
+                            packed_held if m == HELD_TILE else packed,
+                            "w%d" % m,
+                        )
+                    )
+                quantised.append(operands)
+                r += 1
+            if c + CHUNKS_AHEAD < len(CHUNK_WIDTHS):
+                load_chunk(c + CHUNKS_AHEAD)
+
+        for late_round in range(ROUNDS - PASS_LAG, ROUNDS - 1):
+            multiply_round(late_round)
+
+        b_flip = flip_pool.tile([P, P], F32, name="b_flip", tag="x_flip1")
+        nc.tensor.transpose(b_flip[:], b_rows32[:], ident[:])
+        valid_bank = flip_pool.tile([P, ROWS], F32, name="valid_bank", tag="x_flip0")
+        for a in range(ROW_TILES):
+            nc.tensor.matmul(
+                out=valid_bank[:, P * a : P * (a + 1)],
+                lhsT=valid_col[:, a : a + 1].to_broadcast([P, P]),
+                rhs=ident[:],
+                start=True,
+                stop=True,
+            )
+        multiply_round(ROUNDS - 1)
+        for held_round in range(ROUNDS - HELD, ROUNDS):
+            multiply(quantised[held_round], held_round, HELD_TILE)
+
+        bias_col = const.tile([P, ROW_TILES], F32, name="bias_col")
+        nc.scalar.copy(out=bias_col[:], in_=b_flip[:, 0:ROW_TILES])
+        valid = const.tile([P, SAMPLES, TOKENS], F32, name="valid")
+        nc.scalar.copy(out=valid[:].rearrange("p s t -> p (s t)"), in_=valid_bank[:])
+        n_valid = const.tile([P, SAMPLES], F32, name="n_valid")
+        nc.vector.tensor_reduce(out=n_valid[:], in_=valid[:], axis=AX.X, op=ALU.add)
+        n_floor = const.tile([P, 2, SAMPLES], F32, name="n_floor")
+        nc.vector.tensor_scalar_max(out=n_floor[:, 0, :], in0=n_valid[:], scalar1=1.0)
+        nc.vector.tensor_scalar(
+            out=n_floor[:, 1, :], in0=n_valid[:], scalar1=-1.0, scalar2=1.0, op0=ALU.add, op1=ALU.max
+        )
+        n_inverse = const.tile([P, 2, SAMPLES], F32, name="n_inverse")
+        nc.vector.reciprocal(out=n_inverse[:], in_=n_floor[:])
+
+        stats = const.tile([P, SAMPLES, 2, ROW_TILES], F32, name="stats")
+        variance = const.tile([P, SAMPLES, ROW_TILES], F32, name="variance")
+        shape = [P, SAMPLES, TOKENS]
+
+        y = []
+
+        def gelu(m):
+            y_m = tail.tile(shape, F32, name="y%d" % m, bufs=1)
+            nc.scalar.activation(
+                out=y_m[:].rearrange("p s t -> p (s t)"),
+                in_=acc[m][:],
+                func=ACT.Gelu,
+                bias=bias_col[:, m : m + 1],
+            )
+            y.append(y_m)
+
+        for m in range(HELD_TILE):
+            gelu(m)
+
+        def sum_of_squares(squares, m):
+            total_sq = tail.tile([P, SAMPLES], F32, name="total_sq")
+            nc.vector.tensor_reduce(out=total_sq[:], in_=squares[:], axis=AX.X, op=ALU.add)
+            nc.vector.scalar_tensor_tensor(
+                out=variance[:, :, m],
+                in0=total_sq[:],
+                scalar=SQRT_FLOOR,
+                in1=n_inverse[:, 1, :],
+                op0=ALU.max,
+                op1=ALU.mult,
+            )
+
+        squares = [None] * ROW_TILES
+        for m in range(ROW_TILES):
+            kept = tail.tile(shape, F32, name="kept")
+            nc.vector.tensor_tensor(out=kept[:], in0=y[m][:], in1=valid[:], op=ALU.mult)
+            total_y = tail.tile([P, SAMPLES], F32, name="total_y")
+            nc.vector.tensor_reduce(out=total_y[:], in_=kept[:], axis=AX.X, op=ALU.add)
+            mean = stats[:, :, 1, m]
+            nc.vector.tensor_tensor(out=mean, in0=total_y[:], in1=n_inverse[:, 0, :], op=ALU.mult)
+            away = tail.tile(shape, F32, name="away")
+            nc.vector.tensor_tensor(
+                out=away[:], in0=y[m][:], in1=mean.unsqueeze(2).to_broadcast(shape), op=ALU.subtract
+            )
+            away_kept = tail.tile(shape, F32, name="away_kept")
+            nc.vector.tensor_tensor(out=away_kept[:], in0=away[:], in1=valid[:], op=ALU.mult)
+            squares[m] = tail.tile(shape, F32, name="squares")
+            nc.scalar.activation(out=squares[m][:], in_=away_kept[:], func=ACT.Square)
+            if m == HELD_TILE - 2:
+                gelu(HELD_TILE)
+                nc.scalar.activation(out=warm[:, 1:2], in_=one[:], func=ACT.Sqrt)
+            if m > 0:
+                sum_of_squares(squares[m - 1], m - 1)
+        sum_of_squares(squares[ROW_TILES - 1], ROW_TILES - 1)
+
+        root = const.tile([P, SAMPLES, ROW_TILES], F32, name="root")
+        nc.scalar.activation(out=root[:], in_=variance[:], func=ACT.Sqrt)
+        some = const.tile([P, SAMPLES, ROW_TILES], F32, name="some")
+        nc.vector.tensor_single_scalar(out=some[:], in_=variance[:], scalar=SQRT_FLOOR, op=ALU.is_gt)
+        nc.vector.tensor_tensor(out=stats[:, :, 0, :], in0=root[:], in1=some[:], op=ALU.mult)
+
+        stats_bank = flip_pool.tile([P, P], F32, name="stats_bank", tag="w_flip0")
+        nc.tensor.transpose(stats_bank[:], stats[:].rearrange("p s g m -> p (s g m)"), ident[:])
+        result = const.tile([P, P], F32, name="result")
+        nc.vector.tensor_copy(out=result[:], in_=stats_bank[:])
+        nc.sync.dma_start(out=out.rearrange("s (g o) -> (s g) o", o=P), in_=result[:])

@@ -20,14 +20,14 @@ K_PASS = 4 * P
 WORDS_PASS = K_PASS // 2
 ROUNDS = D // K_PASS
 
-CHUNK_MAX = 4 * K_PASS
-CHUNK_WIDTHS = [K_PASS] * 4 + [2 * K_PASS] * 2 + [CHUNK_MAX] * (D // CHUNK_MAX - 2)
-CHUNKS_AHEAD = 3
+CHUNK_ROUNDS = [1, 1, 1, 1] + [2] * 14
+CHUNKS_AHEAD = 4
 
 PASS_LAG = 2
 
-HELD_TILE = ROW_TILES - 1
-HELD = 24
+EARLY_TILES = 2
+LAST_SAMPLES = 8
+FLIP_BANKS = 8 - EARLY_TILES
 
 PAD_WORD = -(1.0 + 49024.0 / 8388608.0)
 SQRT_FLOOR = 2.0 ** -100
@@ -37,7 +37,9 @@ FLOPS = 2 * ROWS * O * D
 
 def tile_linearnnencoder_k_kernel(tc, x, W, b, out):
     nc = tc.nc
-    assert sum(CHUNK_WIDTHS) == D
+    assert sum(CHUNK_ROUNDS) == ROUNDS
+    n_chunks = len(CHUNK_ROUNDS)
+    first_round = [sum(CHUNK_ROUNDS[:c]) for c in range(n_chunks)]
 
     x_rows = x.rearrange("s t k -> (s t) k").rearrange("(a p) k -> p a k", p=P)
     w_rows = W.rearrange("(a p) k -> p a k", p=P)
@@ -45,172 +47,168 @@ def tile_linearnnencoder_k_kernel(tc, x, W, b, out):
     with ExitStack() as ctx:
         ctx.enter_context(tc.manual_schedule())
         const = ctx.enter_context(tc.tile_pool(name="const", bufs=1))
-        natural = ctx.enter_context(tc.tile_pool(name="natural", bufs=CHUNKS_AHEAD))
-        grouped = ctx.enter_context(tc.tile_pool(name="grouped", bufs=2))
-        packed = ctx.enter_context(tc.tile_pool(name="packed", bufs=PASS_LAG + 2))
-        packed_held = ctx.enter_context(tc.tile_pool(name="packed_held", bufs=HELD))
-        scratch = ctx.enter_context(tc.tile_pool(name="scratch", bufs=2))
-        tail = ctx.enter_context(tc.tile_pool(name="tail", bufs=2))
+        packed = ctx.enter_context(tc.tile_pool(name="packed", bufs=ROUNDS))
         acc_pool = ctx.enter_context(tc.psum_pool(name="acc", bufs=1))
-        flip_pool = ctx.enter_context(tc.psum_pool(name="flip", bufs=1))
-
-        chunk_start = [sum(CHUNK_WIDTHS[:c]) for c in range(len(CHUNK_WIDTHS))]
-        chunk_tiles = {}
-
-        def load_chunk(c):
-            k0, width = chunk_start[c], CHUNK_WIDTHS[c]
-            x_nat = natural.tile([P, ROW_TILES, CHUNK_MAX], BF16, name="x_nat")
-            nc.sync.dma_start(out=x_nat[:, :, :width], in_=x_rows[:, :, k0 : k0 + width])
-            w_nat = natural.tile([P, ROW_TILES, CHUNK_MAX], BF16, name="w_nat")
-            nc.sync.dma_start(out=w_nat[:, :, :width], in_=w_rows[:, :, k0 : k0 + width])
-            chunk_tiles[c] = (x_nat, w_nat)
-
-        def as_words(nat):
-            flat = nat[:].rearrange("p a k -> p (a k)").bitcast(F32)
-            return flat.rearrange("p (a w) -> p a w", a=ROW_TILES)
-
-        for c in range(CHUNKS_AHEAD):
-            load_chunk(c)
+        flip_pool = ctx.enter_context(tc.psum_pool(name="flip", bufs=FLIP_BANKS))
 
         ident = const.tile([P, P], F32, name="ident")
-        make_identity(nc, ident[:])
-
         b_rows = const.tile([P, P], BF16, name="b_rows")
-        nc.vector.memset(b_rows[:], 0.0)
-        nc.scalar.dma_start(out=b_rows[0:ROW_TILES, :], in_=b.rearrange("(m o) -> m o", o=P))
         b_rows32 = const.tile([P, P], F32, name="b_rows32")
-        nc.vector.tensor_copy(out=b_rows32[:], in_=b_rows[:])
-
         one = const.tile([P, 1], F32, name="one")
-        nc.vector.memset(one[:], 1.0)
         warm = const.tile([P, 2], F32, name="warm")
-        nc.scalar.activation(out=warm[:, 0:1], in_=one[:], func=ACT.Gelu)
+        differs = const.tile([P, ROW_TILES, WORDS_PASS], F32, name="differs")
+        valid_col = const.tile([P, ROW_TILES], BF16, name="valid_col")
+        ident16 = const.tile([P, P], BF16, name="ident16")
+        bias_col = const.tile([P, ROW_TILES], F32, name="bias_col")
+        acc = [acc_pool.tile([P, ROWS], F32, name="acc%d" % m) for m in range(EARLY_TILES)]
 
-        differing = const.tile([P, ROW_TILES, len(CHUNK_WIDTHS)], F32, name="differing")
-
-        acc = [acc_pool.tile([P, ROWS], F32, name="acc%d" % m) for m in range(ROW_TILES)]
-
-        def flip_rows(words, word0, label):
-            banks = []
-            for half in range(2):
-                bank = flip_pool.tile([P, 2, 2, P], F32, name="%s_flip%d" % (label, half))
-                for i in range(2):
-                    for u in range(2):
-                        nc.tensor.transpose(
-                            bank[:, i, u, :],
-                            words[:, 2 * half + i, word0 + u : word0 + WORDS_PASS : 2],
-                            ident[:],
-                        )
-                banks.append(bank)
-            return banks
-
-        def gather_words(banks, label):
-            rows4 = grouped.tile([P, 4 * ROWS], BF16, name="%s_rows4" % label, align_bytes=64)
-            by_row = rows4[:].bitcast(F32).rearrange("p (a r u) -> p a r u", a=ROW_TILES, u=2)
-            for half in range(2):
-                nc.scalar.copy(
-                    out=by_row[:, 2 * half : 2 * half + 2, :, :],
-                    in_=banks[half][:].rearrange("p i u r -> p i r u"),
-                )
-            return rows4
-
-        def quantise(rows4, n_rows, pool, label):
-            codes = pool.tile([P, n_rows], U32, name="%s_codes" % label, align_bytes=64)
-            scales = pool.tile([P, n_rows], U8, name="%s_scales" % label, align_bytes=64)
-            nc.vector.quantize_mx(out=codes[:].bitcast(FP8X4), scales=scales[:], in_=rows4)
-            return codes, scales
-
-        def multiply(operands, r, m):
+        def multiply(operands, r, m, s0=0, s1=SAMPLES):
             x_codes, x_scales = operands[0]
-            w_codes, w_scales = operands[1 + m]
+            w_codes, w_scales = operands[1 + m // EARLY_TILES]
+            w_cols = slice(P * (m % EARLY_TILES), P * (m % EARLY_TILES + 1))
+            tokens = slice(TOKENS * s0, TOKENS * s1)
             nc.tensor.matmul_mx(
-                out=acc[m][:],
-                lhsT=w_codes[:].bitcast(FP8X4),
-                lhsT_scale=w_scales[:],
-                rhs=x_codes[:].bitcast(FP8X4),
-                rhs_scale=x_scales[:],
+                out=acc[m][:, tokens],
+                lhsT=w_codes[:, w_cols].bitcast(FP8X4),
+                lhsT_scale=w_scales[:, w_cols],
+                rhs=x_codes[:, tokens].bitcast(FP8X4),
+                rhs_scale=x_scales[:, tokens],
                 start=(r == 0),
                 stop=(r == ROUNDS - 1),
             )
 
-        def test_padding(words, c, a):
-            n_words = CHUNK_WIDTHS[c] // 2
-            unequal = scratch.tile([P, CHUNK_MAX // 2], BF16, name="unequal")
-            nc.vector.tensor_scalar(
-                out=unequal[:, :n_words],
-                in0=words[:, a, :n_words],
-                scalar1=PAD_WORD,
-                scalar2=None,
-                op0=ALU.not_equal,
-                op1=ALU.add,
-                accum_out=differing[:, a, c : c + 1],
-            )
-
-        def find_valid_tokens():
-            total = const.tile([P, ROW_TILES], F32, name="total")
-            nc.vector.tensor_reduce(out=total[:], in_=differing[:], axis=AX.X, op=ALU.add)
-            valid_col = const.tile([P, ROW_TILES], F32, name="valid_col")
-            nc.vector.tensor_single_scalar(out=valid_col[:], in_=total[:], scalar=0.0, op=ALU.is_gt)
-            return valid_col
+        quantised = []
 
         def multiply_round(r):
-            for m in range(ROW_TILES):
-                if m != HELD_TILE or r < ROUNDS - HELD:
-                    multiply(quantised[r], r, m)
+            for m in range(EARLY_TILES):
+                multiply(quantised[r], r, m)
 
-        quantised = []
-        r = 0
-        for c in range(len(CHUNK_WIDTHS)):
-            x_words = as_words(chunk_tiles[c][0])
-            w_words = as_words(chunk_tiles[c][1])
-            rounds_here = CHUNK_WIDTHS[c] // K_PASS
-            tests_a_round = ROW_TILES // rounds_here
-            for j in range(rounds_here):
-                x_banks = flip_rows(x_words, WORDS_PASS * j, "x")
-                w_banks = flip_rows(w_words, WORDS_PASS * j, "w")
-                x_rows4 = gather_words(x_banks, "x")
-                w_rows4 = gather_words(w_banks, "w")
-                if r >= PASS_LAG:
-                    multiply_round(r - PASS_LAG)
-                for a in range(tests_a_round * j, tests_a_round * (j + 1)):
-                    test_padding(x_words, c, a)
-                if r == ROUNDS - 1:
-                    valid_col = find_valid_tokens()
-                operands = [quantise(x_rows4[:], ROWS, packed_held, "x")]
-                for m in range(ROW_TILES):
-                    operands.append(
-                        quantise(
-                            w_rows4[:, 4 * P * m : 4 * P * (m + 1)],
-                            P,
-                            packed_held if m == HELD_TILE else packed,
-                            "w%d" % m,
-                        )
+        with ExitStack() as streaming:
+            natural = streaming.enter_context(tc.tile_pool(name="natural", bufs=CHUNKS_AHEAD))
+            grouped = streaming.enter_context(tc.tile_pool(name="grouped", bufs=2))
+
+            x_words = {}
+            w_words = {}
+
+            def as_words(nat):
+                flat = nat[:].rearrange("p a k -> p (a k)").bitcast(F32)
+                return flat.rearrange("p (a w) -> p a w", a=ROW_TILES)
+
+            def load_chunk(c):
+                k0, width = K_PASS * first_round[c], K_PASS * CHUNK_ROUNDS[c]
+                x_nat = natural.tile([P, ROW_TILES, width], BF16, name="x_nat")
+                nc.sync.dma_start(out=x_nat[:], in_=x_rows[:, :, k0 : k0 + width])
+                w_nat = natural.tile([P, ROW_TILES, width], BF16, name="w_nat")
+                nc.sync.dma_start(out=w_nat[:], in_=w_rows[:, :, k0 : k0 + width])
+                x_words[c] = as_words(x_nat)
+                w_words[c] = as_words(w_nat)
+
+            for c in range(CHUNKS_AHEAD):
+                load_chunk(c)
+
+            make_identity(nc, ident[:])
+            nc.vector.memset(differs[:], 0.0)
+            nc.vector.memset(b_rows[:], 0.0)
+            nc.scalar.dma_start(out=b_rows[0:ROW_TILES, :], in_=b.rearrange("(m o) -> m o", o=P))
+            nc.vector.tensor_copy(out=b_rows32[:], in_=b_rows[:])
+            nc.vector.tensor_copy(out=ident16[:], in_=ident[:])
+            nc.vector.memset(one[:], 1.0)
+            nc.scalar.activation(out=warm[:, 0:1], in_=one[:], func=ACT.Gelu)
+
+            def flip_rows(words):
+                banks = []
+                for half in range(2):
+                    bank = flip_pool.tile([P, 2, 2, P], F32, name="flip")
+                    for i in range(2):
+                        for u in range(2):
+                            nc.tensor.transpose(
+                                bank[:, i, u, :], words[:, 2 * half + i, u : WORDS_PASS : 2], ident[:]
+                            )
+                    banks.append(bank)
+                return banks
+
+            def gather_words(banks, label):
+                rows4 = grouped.tile([P, 4 * ROWS], BF16, name="%s_rows4" % label, align_bytes=64)
+                by_row = rows4[:].bitcast(F32).rearrange("p (a r u) -> p a r u", a=ROW_TILES, u=2)
+                for half in range(2):
+                    nc.scalar.copy(
+                        out=by_row[:, 2 * half : 2 * half + 2, :, :],
+                        in_=banks[half][:].rearrange("p i u r -> p i r u"),
                     )
-                quantised.append(operands)
-                r += 1
-            if c + CHUNKS_AHEAD < len(CHUNK_WIDTHS):
-                load_chunk(c + CHUNKS_AHEAD)
+                return rows4
 
-        for late_round in range(ROUNDS - PASS_LAG, ROUNDS - 1):
+            def quantise(rows4, n_rows, bufs, label):
+                codes = packed.tile(
+                    [P, n_rows], U32, name="%s_codes" % label, align_bytes=64, bufs=bufs
+                )
+                scales = packed.tile(
+                    [P, n_rows], U8, name="%s_scales" % label, align_bytes=64, bufs=bufs
+                )
+                nc.vector.quantize_mx(out=codes[:].bitcast(FP8X4), scales=scales[:], in_=rows4)
+                return codes, scales
+
+            r = 0
+            for c in range(n_chunks):
+                for j in range(CHUNK_ROUNDS[c]):
+                    here = slice(WORDS_PASS * j, WORDS_PASS * (j + 1))
+                    nc.vector.scalar_tensor_tensor(
+                        out=differs[:],
+                        in0=x_words[c][:, :, here],
+                        scalar=PAD_WORD,
+                        in1=differs[:],
+                        op0=ALU.not_equal,
+                        op1=ALU.max,
+                    )
+                    x_banks = flip_rows(x_words[c][:, :, here])
+                    w_banks = flip_rows(w_words[c][:, :, here])
+                    x_rows4 = gather_words(x_banks, "x")
+                    w_rows4 = gather_words(w_banks, "w")
+                    if r >= PASS_LAG:
+                        multiply_round(r - PASS_LAG)
+                    if r == ROUNDS - 1:
+                        nc.vector.tensor_reduce(
+                            out=valid_col[:], in_=differs[:], axis=AX.X, op=ALU.max
+                        )
+                    split = 4 * P * EARLY_TILES
+                    quantised.append(
+                        [
+                            quantise(x_rows4[:], ROWS, ROUNDS, "x"),
+                            quantise(w_rows4[:, :split], P * EARLY_TILES, PASS_LAG + 2, "w_early"),
+                            quantise(
+                                w_rows4[:, split:], P * (ROW_TILES - EARLY_TILES), ROUNDS, "w_late"
+                            ),
+                        ]
+                    )
+                    r += 1
+                if c + CHUNKS_AHEAD < n_chunks:
+                    load_chunk(c + CHUNKS_AHEAD)
+
+        for late_round in range(ROUNDS - PASS_LAG, ROUNDS):
             multiply_round(late_round)
 
-        b_flip = flip_pool.tile([P, P], F32, name="b_flip", tag="x_flip1")
+        b_flip = flip_pool.tile([P, P], F32, name="b_flip", tag="flip")
         nc.tensor.transpose(b_flip[:], b_rows32[:], ident[:])
-        valid_bank = flip_pool.tile([P, ROWS], F32, name="valid_bank", tag="x_flip0")
+        nc.scalar.copy(out=bias_col[:], in_=b_flip[:, 0:ROW_TILES])
+        valid_bank = flip_pool.tile([P, ROWS], F32, name="valid_bank", tag="flip")
         for a in range(ROW_TILES):
             nc.tensor.matmul(
                 out=valid_bank[:, P * a : P * (a + 1)],
                 lhsT=valid_col[:, a : a + 1].to_broadcast([P, P]),
-                rhs=ident[:],
+                rhs=ident16[:],
                 start=True,
                 stop=True,
             )
-        multiply_round(ROUNDS - 1)
-        for held_round in range(ROUNDS - HELD, ROUNDS):
-            multiply(quantised[held_round], held_round, HELD_TILE)
 
-        bias_col = const.tile([P, ROW_TILES], F32, name="bias_col")
-        nc.scalar.copy(out=bias_col[:], in_=b_flip[:, 0:ROW_TILES])
+        units = [(m, 0, SAMPLES) for m in range(ROW_TILES - 1)]
+        units += [(ROW_TILES - 1, s0, s0 + LAST_SAMPLES) for s0 in range(0, SAMPLES, LAST_SAMPLES)]
+        for m in range(EARLY_TILES, ROW_TILES):
+            acc.append(flip_pool.tile([P, ROWS], F32, name="acc%d" % m, tag="flip"))
+        for m, s0, s1 in units:
+            if m >= EARLY_TILES:
+                for r in range(ROUNDS):
+                    multiply(quantised[r], r, m, s0, s1)
+
+        tail = ctx.enter_context(tc.tile_pool(name="tail", bufs=2))
         valid = const.tile([P, SAMPLES, TOKENS], F32, name="valid")
         nc.scalar.copy(out=valid[:].rearrange("p s t -> p (s t)"), in_=valid_bank[:])
         n_valid = const.tile([P, SAMPLES], F32, name="n_valid")
@@ -222,68 +220,63 @@ def tile_linearnnencoder_k_kernel(tc, x, W, b, out):
         )
         n_inverse = const.tile([P, 2, SAMPLES], F32, name="n_inverse")
         nc.vector.reciprocal(out=n_inverse[:], in_=n_floor[:])
+        weight = const.tile([P, 2, SAMPLES, TOKENS], F32, name="weight")
+        for g in range(2):
+            nc.vector.tensor_tensor(
+                out=weight[:, g],
+                in0=valid[:],
+                in1=n_inverse[:, g, :].unsqueeze(2).to_broadcast([P, SAMPLES, TOKENS]),
+                op=ALU.mult,
+            )
 
         stats = const.tile([P, SAMPLES, 2, ROW_TILES], F32, name="stats")
         variance = const.tile([P, SAMPLES, ROW_TILES], F32, name="variance")
-        shape = [P, SAMPLES, TOKENS]
-
         y = []
 
-        def gelu(m):
-            y_m = tail.tile(shape, F32, name="y%d" % m, bufs=1)
+        def gelu(unit):
+            m, s0, s1 = unit
+            y_u = tail.tile([P, s1 - s0, TOKENS], F32, name="y", bufs=len(units))
             nc.scalar.activation(
-                out=y_m[:].rearrange("p s t -> p (s t)"),
-                in_=acc[m][:],
+                out=y_u[:].rearrange("p s t -> p (s t)"),
+                in_=acc[m][:, TOKENS * s0 : TOKENS * s1],
                 func=ACT.Gelu,
                 bias=bias_col[:, m : m + 1],
             )
-            y.append(y_m)
+            y.append(y_u)
 
-        for m in range(HELD_TILE):
-            gelu(m)
+        for unit in units:
+            gelu(unit)
+        nc.scalar.activation(out=warm[:, 1:2], in_=one[:], func=ACT.Sqrt)
 
-        def sum_of_squares(squares, m):
-            total_sq = tail.tile([P, SAMPLES], F32, name="total_sq")
-            nc.vector.tensor_reduce(out=total_sq[:], in_=squares[:], axis=AX.X, op=ALU.add)
-            nc.vector.scalar_tensor_tensor(
-                out=variance[:, :, m],
-                in0=total_sq[:],
-                scalar=SQRT_FLOOR,
-                in1=n_inverse[:, 1, :],
-                op0=ALU.max,
-                op1=ALU.mult,
-            )
-
-        squares = [None] * ROW_TILES
-        for m in range(ROW_TILES):
-            kept = tail.tile(shape, F32, name="kept")
-            nc.vector.tensor_tensor(out=kept[:], in0=y[m][:], in1=valid[:], op=ALU.mult)
-            total_y = tail.tile([P, SAMPLES], F32, name="total_y")
-            nc.vector.tensor_reduce(out=total_y[:], in_=kept[:], axis=AX.X, op=ALU.add)
-            mean = stats[:, :, 1, m]
-            nc.vector.tensor_tensor(out=mean, in0=total_y[:], in1=n_inverse[:, 0, :], op=ALU.mult)
+        for i, (m, s0, s1) in enumerate(units):
+            shape = [P, s1 - s0, TOKENS]
+            share = tail.tile(shape, F32, name="share")
+            nc.vector.tensor_tensor(out=share[:], in0=y[i][:], in1=weight[:, 0, s0:s1, :], op=ALU.mult)
+            mean = stats[:, s0:s1, 1, m]
+            nc.vector.tensor_reduce(out=mean, in_=share[:], axis=AX.X, op=ALU.add)
             away = tail.tile(shape, F32, name="away")
             nc.vector.tensor_tensor(
-                out=away[:], in0=y[m][:], in1=mean.unsqueeze(2).to_broadcast(shape), op=ALU.subtract
+                out=away[:], in0=y[i][:], in1=mean.unsqueeze(2).to_broadcast(shape), op=ALU.subtract
             )
-            away_kept = tail.tile(shape, F32, name="away_kept")
-            nc.vector.tensor_tensor(out=away_kept[:], in0=away[:], in1=valid[:], op=ALU.mult)
-            squares[m] = tail.tile(shape, F32, name="squares")
-            nc.scalar.activation(out=squares[m][:], in_=away_kept[:], func=ACT.Square)
-            if m == HELD_TILE - 2:
-                gelu(HELD_TILE)
-                nc.scalar.activation(out=warm[:, 1:2], in_=one[:], func=ACT.Sqrt)
-            if m > 0:
-                sum_of_squares(squares[m - 1], m - 1)
-        sum_of_squares(squares[ROW_TILES - 1], ROW_TILES - 1)
+            away_share = tail.tile(shape, F32, name="away_share")
+            nc.vector.tensor_tensor(
+                out=away_share[:], in0=away[:], in1=weight[:, 1, s0:s1, :], op=ALU.mult
+            )
+            square_share = tail.tile(shape, F32, name="square_share")
+            nc.vector.tensor_tensor(
+                out=square_share[:], in0=away_share[:], in1=away[:], op=ALU.mult
+            )
+            nc.vector.tensor_reduce(
+                out=variance[:, s0:s1, m], in_=square_share[:], axis=AX.X, op=ALU.add
+            )
 
         root = const.tile([P, SAMPLES, ROW_TILES], F32, name="root")
-        nc.scalar.activation(out=root[:], in_=variance[:], func=ACT.Sqrt)
+        nc.scalar.activation(out=root[:], in_=variance[:], func=ACT.Sqrt, bias=SQRT_FLOOR)
         some = const.tile([P, SAMPLES, ROW_TILES], F32, name="some")
-        nc.vector.tensor_single_scalar(out=some[:], in_=variance[:], scalar=SQRT_FLOOR, op=ALU.is_gt)
+        nc.vector.tensor_single_scalar(out=some[:], in_=variance[:], scalar=0.0, op=ALU.is_gt)
         nc.vector.tensor_tensor(out=stats[:, :, 0, :], in0=root[:], in1=some[:], op=ALU.mult)
 
-        stats_bank = flip_pool.tile([P, P], F32, name="stats_bank", tag="w_flip0")
+        stats_bank = flip_pool.tile([P, P], F32, name="stats_bank", tag="flip")
         nc.tensor.transpose(stats_bank[:], stats[:].rearrange("p s g m -> p (s g m)"), ident[:])
         result = const.tile([P, P], F32, name="result")
         nc.vector.tensor_copy(out=result[:], in_=stats_bank[:])

@@ -28,6 +28,7 @@ PASS_LAG = 2
 EARLY_TILES = 2
 LAST_SAMPLES = 8
 FLIP_BANKS = 8 - EARLY_TILES
+FILL_PASSES = 12
 
 PAD_WORD = -(1.0 + 49024.0 / 8388608.0)
 SQRT_FLOOR = 2.0 ** -100
@@ -97,9 +98,13 @@ def tile_linearnnencoder_k_kernel(tc, x, W, b, out):
             def load_chunk(c):
                 k0, width = K_PASS * first_round[c], K_PASS * CHUNK_ROUNDS[c]
                 x_nat = natural.tile([P, ROW_TILES, width], BF16, name="x_nat")
-                nc.sync.dma_start(out=x_nat[:], in_=x_rows[:, :, k0 : k0 + width])
                 w_nat = natural.tile([P, ROW_TILES, width], BF16, name="w_nat")
-                nc.sync.dma_start(out=w_nat[:], in_=w_rows[:, :, k0 : k0 + width])
+                step = ROW_TILES // 2 if c == 0 else ROW_TILES
+                for nat, rows in ((x_nat, x_rows), (w_nat, w_rows)):
+                    for a in range(0, ROW_TILES, step):
+                        nc.sync.dma_start(
+                            out=nat[:, a : a + step, :], in_=rows[:, a : a + step, k0 : k0 + width]
+                        )
                 x_words[c] = as_words(x_nat)
                 w_words[c] = as_words(w_nat)
 
@@ -183,7 +188,7 @@ def tile_linearnnencoder_k_kernel(tc, x, W, b, out):
                 if c + CHUNKS_AHEAD < n_chunks:
                     load_chunk(c + CHUNKS_AHEAD)
 
-        for late_round in range(ROUNDS - PASS_LAG, ROUNDS):
+        for late_round in range(ROUNDS - PASS_LAG, ROUNDS - 1):
             multiply_round(late_round)
 
         b_flip = flip_pool.tile([P, P], F32, name="b_flip", tag="flip")
@@ -203,10 +208,14 @@ def tile_linearnnencoder_k_kernel(tc, x, W, b, out):
         units += [(ROW_TILES - 1, s0, s0 + LAST_SAMPLES) for s0 in range(0, SAMPLES, LAST_SAMPLES)]
         for m in range(EARLY_TILES, ROW_TILES):
             acc.append(flip_pool.tile([P, ROWS], F32, name="acc%d" % m, tag="flip"))
-        for m, s0, s1 in units:
-            if m >= EARLY_TILES:
-                for r in range(ROUNDS):
-                    multiply(quantised[r], r, m, s0, s1)
+        for r in range(FILL_PASSES):
+            multiply(quantised[r], r, EARLY_TILES)
+        multiply_round(ROUNDS - 1)
+        for r in range(FILL_PASSES, ROUNDS):
+            multiply(quantised[r], r, EARLY_TILES)
+        for m, s0, s1 in units[EARLY_TILES + 1 :]:
+            for r in range(ROUNDS):
+                multiply(quantised[r], r, m, s0, s1)
 
         tail = ctx.enter_context(tc.tile_pool(name="tail", bufs=2))
         valid = const.tile([P, SAMPLES, TOKENS], F32, name="valid")

@@ -28,7 +28,7 @@ PASS_LAG = 2
 EARLY_TILES = 2
 LAST_SAMPLES = 8
 FLIP_BANKS = 8 - EARLY_TILES
-FILL_PASSES = 12
+FILL_PASSES = 10
 
 PAD_WORD = -(1.0 + 49024.0 / 8388608.0)
 SQRT_FLOOR = 2.0 ** -100
@@ -253,31 +253,79 @@ def tile_linearnnencoder_k_kernel(tc, x, W, b, out):
             )
             y.append(y_u)
 
-        for unit in units:
-            gelu(unit)
-        nc.scalar.activation(out=warm[:, 1:2], in_=one[:], func=ACT.Sqrt)
+        away = {}
+        squares = {}
 
-        for i, (m, s0, s1) in enumerate(units):
-            shape = [P, s1 - s0, TOKENS]
-            share = tail.tile(shape, F32, name="share")
+        def find_share(i):
+            m, s0, s1 = units[i]
+            share = tail.tile([P, s1 - s0, TOKENS], F32, name="share")
             nc.vector.tensor_tensor(out=share[:], in0=y[i][:], in1=weight[:, 0, s0:s1, :], op=ALU.mult)
-            mean = stats[:, s0:s1, 1, m]
-            nc.vector.tensor_reduce(out=mean, in_=share[:], axis=AX.X, op=ALU.add)
-            away = tail.tile(shape, F32, name="away")
+            return share
+
+        def find_mean(i, share):
+            m, s0, s1 = units[i]
+            nc.vector.tensor_reduce(out=stats[:, s0:s1, 1, m], in_=share[:], axis=AX.X, op=ALU.add)
+
+        def find_away(i):
+            m, s0, s1 = units[i]
+            shape = [P, s1 - s0, TOKENS]
+            away[i] = tail.tile(shape, F32, name="away")
             nc.vector.tensor_tensor(
-                out=away[:], in0=y[i][:], in1=mean.unsqueeze(2).to_broadcast(shape), op=ALU.subtract
+                out=away[i][:],
+                in0=y[i][:],
+                in1=stats[:, s0:s1, 1, m].unsqueeze(2).to_broadcast(shape),
+                op=ALU.subtract,
             )
-            away_share = tail.tile(shape, F32, name="away_share")
-            nc.vector.tensor_tensor(
-                out=away_share[:], in0=away[:], in1=weight[:, 1, s0:s1, :], op=ALU.mult
-            )
+
+        def square_on_scalar(i):
+            m, s0, s1 = units[i]
+            squares[i] = tail.tile([P, s1 - s0, TOKENS], F32, name="squares")
+            nc.scalar.activation(out=squares[i][:], in_=away[i][:], func=ACT.Square)
+
+        def find_square_share(i):
+            m, s0, s1 = units[i]
+            shape = [P, s1 - s0, TOKENS]
+            first = squares.get(i)
+            if first is None:
+                first = tail.tile(shape, F32, name="away_share")
+                nc.vector.tensor_tensor(
+                    out=first[:], in0=away[i][:], in1=weight[:, 1, s0:s1, :], op=ALU.mult
+                )
+                second = away[i][:]
+            else:
+                second = weight[:, 1, s0:s1, :]
             square_share = tail.tile(shape, F32, name="square_share")
-            nc.vector.tensor_tensor(
-                out=square_share[:], in0=away_share[:], in1=away[:], op=ALU.mult
-            )
+            nc.vector.tensor_tensor(out=square_share[:], in0=first[:], in1=second, op=ALU.mult)
+            return square_share
+
+        def find_variance(i, square_share):
+            m, s0, s1 = units[i]
             nc.vector.tensor_reduce(
                 out=variance[:, s0:s1, m], in_=square_share[:], axis=AX.X, op=ALU.add
             )
+
+        early = list(range(EARLY_TILES))
+        for i in early:
+            gelu(units[i])
+        shares = [find_share(i) for i in early]
+        for i in early:
+            find_mean(i, shares[i])
+        for i in early:
+            find_away(i)
+            square_on_scalar(i)
+        gelu(units[EARLY_TILES])
+        square_shares = [find_square_share(i) for i in early]
+        for i in early:
+            find_variance(i, square_shares[i])
+        for i in range(EARLY_TILES, len(units)):
+            find_mean(i, find_share(i))
+            find_away(i)
+            if i + 1 < len(units):
+                gelu(units[i + 1])
+            if i == EARLY_TILES:
+                square_on_scalar(i)
+            find_variance(i, find_square_share(i))
+        nc.scalar.activation(out=warm[:, 1:2], in_=one[:], func=ACT.Sqrt)
 
         root = const.tile([P, SAMPLES, ROW_TILES], F32, name="root")
         nc.scalar.activation(out=root[:], in_=variance[:], func=ACT.Sqrt, bias=SQRT_FLOOR)

@@ -28,7 +28,7 @@ PASS_LAG = 2
 EARLY_TILES = 2
 LAST_SAMPLES = 8
 FLIP_BANKS = 8 - EARLY_TILES
-FILL_PASSES = 10
+FILL_PASSES = 12
 
 PAD_WORD = -(1.0 + 49024.0 / 8388608.0)
 SQRT_FLOOR = 2.0 ** -100
@@ -320,10 +320,10 @@ def tile_linearnnencoder_k_kernel(tc, x, W, b, out):
         for i in range(EARLY_TILES, len(units)):
             find_mean(i, find_share(i))
             find_away(i)
-            if i + 1 < len(units):
-                gelu(units[i + 1])
             if i == EARLY_TILES:
                 square_on_scalar(i)
+            if i + 1 < len(units):
+                gelu(units[i + 1])
             find_variance(i, find_square_share(i))
         nc.scalar.activation(out=warm[:, 1:2], in_=one[:], func=ACT.Sqrt)
 

@@ -284,18 +284,10 @@ def tile_linearnnencoder_k_kernel(tc, x, W, b, out):
 
         def find_square_share(i):
             m, s0, s1 = units[i]
-            shape = [P, s1 - s0, TOKENS]
-            first = squares.get(i)
-            if first is None:
-                first = tail.tile(shape, F32, name="away_share")
-                nc.vector.tensor_tensor(
-                    out=first[:], in0=away[i][:], in1=weight[:, 1, s0:s1, :], op=ALU.mult
-                )
-                second = away[i][:]
-            else:
-                second = weight[:, 1, s0:s1, :]
-            square_share = tail.tile(shape, F32, name="square_share")
-            nc.vector.tensor_tensor(out=square_share[:], in0=first[:], in1=second, op=ALU.mult)
+            square_share = tail.tile([P, s1 - s0, TOKENS], F32, name="square_share")
+            nc.vector.tensor_tensor(
+                out=square_share[:], in0=squares[i][:], in1=weight[:, 1, s0:s1, :], op=ALU.mult
+            )
             return square_share
 
         def find_variance(i, square_share):
@@ -317,14 +309,48 @@ def tile_linearnnencoder_k_kernel(tc, x, W, b, out):
         square_shares = [find_square_share(i) for i in early]
         for i in early:
             find_variance(i, square_shares[i])
-        for i in range(EARLY_TILES, len(units)):
+        for i in range(EARLY_TILES, ROW_TILES - 1):
             find_mean(i, find_share(i))
             find_away(i)
-            if i == EARLY_TILES:
-                square_on_scalar(i)
+            square_on_scalar(i)
+            gelu(units[i + 1])
+            find_variance(i, find_square_share(i))
+
+        for i in range(ROW_TILES - 1, len(units)):
+            m, s0, s1 = units[i]
             if i + 1 < len(units):
                 gelu(units[i + 1])
-            find_variance(i, find_square_share(i))
+            spare = tail.tile([P, s1 - s0, TOKENS], F32, name="spare")
+            away_share = tail.tile([P, s1 - s0, TOKENS], F32, name="away_share")
+            for s in range(s0, s1):
+                nc.vector.scalar_tensor_tensor(
+                    out=spare[:, s - s0, :],
+                    in0=y[i][:, s - s0, :],
+                    scalar=1.0,
+                    in1=weight[:, 0, s, :],
+                    op0=ALU.mult,
+                    op1=ALU.mult,
+                    accum_out=stats[:, s : s + 1, 1, m],
+                )
+            for s in range(s0, s1):
+                nc.vector.scalar_tensor_tensor(
+                    out=away_share[:, s - s0, :],
+                    in0=y[i][:, s - s0, :],
+                    scalar=stats[:, s : s + 1, 1, m],
+                    in1=weight[:, 1, s, :],
+                    op0=ALU.subtract,
+                    op1=ALU.mult,
+                )
+            for s in range(s0, s1):
+                nc.vector.scalar_tensor_tensor(
+                    out=spare[:, s - s0, :],
+                    in0=y[i][:, s - s0, :],
+                    scalar=stats[:, s : s + 1, 1, m],
+                    in1=away_share[:, s - s0, :],
+                    op0=ALU.subtract,
+                    op1=ALU.mult,
+                    accum_out=variance[:, s : s + 1, m],
+                )
         nc.scalar.activation(out=warm[:, 1:2], in_=one[:], func=ACT.Sqrt)
 
         root = const.tile([P, SAMPLES, ROW_TILES], F32, name="root")

@@ -20,15 +20,17 @@ K_PASS = 4 * P
 WORDS_PASS = K_PASS // 2
 ROUNDS = D // K_PASS
 
-CHUNK_ROUNDS = [1, 1, 1, 1] + [2] * 14
+CHUNK_ROUNDS = [1] * 8 + [2] * 12
 CHUNKS_AHEAD = 4
 
-PASS_LAG = 2
+PASS_LAG = 3
 
 EARLY_TILES = 2
-LAST_SAMPLES = 8
+LAST_GROUPS = [8, 8]
 FLIP_BANKS = 8 - EARLY_TILES
 FILL_PASSES = 12
+
+SETTLED_ROUND = 6
 
 PAD_WORD = -(1.0 + 49024.0 / 8388608.0)
 SQRT_FLOOR = 2.0 ** -100
@@ -63,13 +65,20 @@ def tile_linearnnencoder_k_kernel(tc, x, W, b, out):
         bias_col = const.tile([P, ROW_TILES], F32, name="bias_col")
         acc = [acc_pool.tile([P, ROWS], F32, name="acc%d" % m) for m in range(EARLY_TILES)]
 
+        last_banks = {}
+
+        def sums_of(m, s0, s1):
+            if m == ROW_TILES - 1:
+                return last_banks[s0][:]
+            return acc[m][:, TOKENS * s0 : TOKENS * s1]
+
         def multiply(operands, r, m, s0=0, s1=SAMPLES):
             x_codes, x_scales = operands[0]
             w_codes, w_scales = operands[1 + m // EARLY_TILES]
             w_cols = slice(P * (m % EARLY_TILES), P * (m % EARLY_TILES + 1))
             tokens = slice(TOKENS * s0, TOKENS * s1)
             nc.tensor.matmul_mx(
-                out=acc[m][:, tokens],
+                out=sums_of(m, s0, s1),
                 lhsT=w_codes[:, w_cols].bitcast(FP8X4),
                 lhsT_scale=w_scales[:, w_cols],
                 rhs=x_codes[:, tokens].bitcast(FP8X4),
@@ -86,7 +95,7 @@ def tile_linearnnencoder_k_kernel(tc, x, W, b, out):
 
         with ExitStack() as streaming:
             natural = streaming.enter_context(tc.tile_pool(name="natural", bufs=CHUNKS_AHEAD))
-            grouped = streaming.enter_context(tc.tile_pool(name="grouped", bufs=2))
+            grouped = streaming.enter_context(tc.tile_pool(name="grouped", bufs=3))
 
             x_words = {}
             w_words = {}
@@ -112,13 +121,11 @@ def tile_linearnnencoder_k_kernel(tc, x, W, b, out):
                 load_chunk(c)
 
             make_identity(nc, ident[:])
+            nc.vector.memset(one[:], 1.0)
+            nc.scalar.activation(out=warm[:, 0:1], in_=one[:], func=ACT.Gelu)
             nc.vector.memset(differs[:], 0.0)
             nc.vector.memset(b_rows[:], 0.0)
             nc.scalar.dma_start(out=b_rows[0:ROW_TILES, :], in_=b.rearrange("(m o) -> m o", o=P))
-            nc.vector.tensor_copy(out=b_rows32[:], in_=b_rows[:])
-            nc.vector.tensor_copy(out=ident16[:], in_=ident[:])
-            nc.vector.memset(one[:], 1.0)
-            nc.scalar.activation(out=warm[:, 0:1], in_=one[:], func=ACT.Gelu)
 
             def flip_rows(words):
                 banks = []
@@ -156,6 +163,9 @@ def tile_linearnnencoder_k_kernel(tc, x, W, b, out):
             for c in range(n_chunks):
                 for j in range(CHUNK_ROUNDS[c]):
                     here = slice(WORDS_PASS * j, WORDS_PASS * (j + 1))
+                    if r == SETTLED_ROUND:
+                        nc.vector.tensor_copy(out=b_rows32[:], in_=b_rows[:])
+                        nc.vector.tensor_copy(out=ident16[:], in_=ident[:])
                     nc.vector.scalar_tensor_tensor(
                         out=differs[:],
                         in0=x_words[c][:, :, here],
@@ -205,9 +215,14 @@ def tile_linearnnencoder_k_kernel(tc, x, W, b, out):
             )
 
         units = [(m, 0, SAMPLES) for m in range(ROW_TILES - 1)]
-        units += [(ROW_TILES - 1, s0, s0 + LAST_SAMPLES) for s0 in range(0, SAMPLES, LAST_SAMPLES)]
-        for m in range(EARLY_TILES, ROW_TILES):
+        for g in range(len(LAST_GROUPS)):
+            units.append((ROW_TILES - 1, sum(LAST_GROUPS[:g]), sum(LAST_GROUPS[: g + 1])))
+        for m in range(EARLY_TILES, ROW_TILES - 1):
             acc.append(flip_pool.tile([P, ROWS], F32, name="acc%d" % m, tag="flip"))
+        for m, s0, s1 in units[ROW_TILES - 1 :]:
+            last_banks[s0] = flip_pool.tile(
+                [P, TOKENS * (s1 - s0)], F32, name="last%d" % s0, tag="flip"
+            )
         for r in range(FILL_PASSES):
             multiply(quantised[r], r, EARLY_TILES)
         multiply_round(ROUNDS - 1)
@@ -247,7 +262,7 @@ def tile_linearnnencoder_k_kernel(tc, x, W, b, out):
             y_u = tail.tile([P, s1 - s0, TOKENS], F32, name="y", bufs=len(units))
             nc.scalar.activation(
                 out=y_u[:].rearrange("p s t -> p (s t)"),
-                in_=acc[m][:, TOKENS * s0 : TOKENS * s1],
+                in_=sums_of(m, s0, s1),
                 func=ACT.Gelu,
                 bias=bias_col[:, m : m + 1],
             )

@@ -23,6 +23,9 @@ ROUNDS = D // K_PASS
 CHUNK_ROUNDS = [1] * 8 + [2] * 12
 CHUNKS_AHEAD = 4
 
+SORTED_TILE = 3
+FIRST_SORTED = 8
+
 PASS_LAG = 3
 
 EARLY_TILES = 2
@@ -95,10 +98,12 @@ def tile_linearnnencoder_k_kernel(tc, x, W, b, out):
 
         with ExitStack() as streaming:
             natural = streaming.enter_context(tc.tile_pool(name="natural", bufs=CHUNKS_AHEAD))
+            sorted_pool = streaming.enter_context(tc.tile_pool(name="sorted", bufs=2))
             grouped = streaming.enter_context(tc.tile_pool(name="grouped", bufs=3))
 
             x_words = {}
             w_words = {}
+            w_sorted = {}
 
             def as_words(nat):
                 flat = nat[:].rearrange("p a k -> p (a k)").bitcast(F32)
@@ -127,15 +132,21 @@ def tile_linearnnencoder_k_kernel(tc, x, W, b, out):
             nc.vector.memset(b_rows[:], 0.0)
             nc.scalar.dma_start(out=b_rows[0:ROW_TILES, :], in_=b.rearrange("(m o) -> m o", o=P))
 
-            def flip_rows(words):
+            def sort_words(c):
+                tile_c = sorted_pool.tile([P, K_PASS * CHUNK_ROUNDS[c]], BF16, name="w_sorted")
+                w_sorted[c] = tile_c[:].bitcast(F32).rearrange("p (j u q) -> p j u q", u=2, q=P)
+                nc.vector.tensor_copy(
+                    out=w_sorted[c],
+                    in_=w_words[c][:, SORTED_TILE, :].rearrange("p (j q u) -> p j u q", u=2, q=P),
+                )
+
+            def flip_rows(columns):
                 banks = []
                 for half in range(2):
                     bank = flip_pool.tile([P, 2, 2, P], F32, name="flip")
                     for i in range(2):
                         for u in range(2):
-                            nc.tensor.transpose(
-                                bank[:, i, u, :], words[:, 2 * half + i, u : WORDS_PASS : 2], ident[:]
-                            )
+                            nc.tensor.transpose(bank[:, i, u, :], columns(2 * half + i, u), ident[:])
                     banks.append(bank)
                 return banks
 
@@ -174,8 +185,16 @@ def tile_linearnnencoder_k_kernel(tc, x, W, b, out):
                         op0=ALU.not_equal,
                         op1=ALU.max,
                     )
-                    x_banks = flip_rows(x_words[c][:, :, here])
-                    w_banks = flip_rows(w_words[c][:, :, here])
+                    if j == 0 and FIRST_SORTED <= c + 1 < n_chunks:
+                        sort_words(c + 1)
+                    x_banks = flip_rows(
+                        lambda a, u: x_words[c][:, a, WORDS_PASS * j + u : WORDS_PASS * (j + 1) : 2]
+                    )
+                    w_banks = flip_rows(
+                        lambda a, u: w_sorted[c][:, j, u, :]
+                        if a == SORTED_TILE and c in w_sorted
+                        else w_words[c][:, a, WORDS_PASS * j + u : WORDS_PASS * (j + 1) : 2]
+                    )
                     x_rows4 = gather_words(x_banks, "x")
                     w_rows4 = gather_words(w_banks, "w")
                     if r >= PASS_LAG:

@@ -23,8 +23,11 @@ ROUNDS = D // K_PASS
 CHUNK_ROUNDS = [1] * 8 + [2] * 12
 CHUNKS_AHEAD = 4
 
-SORTED_TILE = 3
+FIRST_SORTED_TILE = 1
+SORTED_TILES = 4 - FIRST_SORTED_TILE
 FIRST_SORTED = 8
+
+VECTOR_TESTS = 3
 
 PASS_LAG = 3
 
@@ -62,7 +65,9 @@ def tile_linearnnencoder_k_kernel(tc, x, W, b, out):
         b_rows32 = const.tile([P, P], F32, name="b_rows32")
         one = const.tile([P, 1], F32, name="one")
         warm = const.tile([P, 2], F32, name="warm")
-        differs = const.tile([P, ROW_TILES, WORDS_PASS], F32, name="differs")
+        differs = const.tile([P, VECTOR_TESTS, WORDS_PASS], F32, name="differs")
+        distance = const.tile([P, n_chunks], F32, name="distance")
+        distance_all = const.tile([P, 1], F32, name="distance_all")
         valid_col = const.tile([P, ROW_TILES], BF16, name="valid_col")
         ident16 = const.tile([P, P], BF16, name="ident16")
         bias_col = const.tile([P, ROW_TILES], F32, name="bias_col")
@@ -103,6 +108,7 @@ def tile_linearnnencoder_k_kernel(tc, x, W, b, out):
 
             x_words = {}
             w_words = {}
+            w_flat = {}
             w_sorted = {}
 
             def as_words(nat):
@@ -121,6 +127,7 @@ def tile_linearnnencoder_k_kernel(tc, x, W, b, out):
                         )
                 x_words[c] = as_words(x_nat)
                 w_words[c] = as_words(w_nat)
+                w_flat[c] = w_nat[:].rearrange("p a k -> p (a k)").bitcast(F32)
 
             for c in range(CHUNKS_AHEAD):
                 load_chunk(c)
@@ -133,11 +140,28 @@ def tile_linearnnencoder_k_kernel(tc, x, W, b, out):
             nc.scalar.dma_start(out=b_rows[0:ROW_TILES, :], in_=b.rearrange("(m o) -> m o", o=P))
 
             def sort_words(c):
-                tile_c = sorted_pool.tile([P, K_PASS * CHUNK_ROUNDS[c]], BF16, name="w_sorted")
-                w_sorted[c] = tile_c[:].bitcast(F32).rearrange("p (j u q) -> p j u q", u=2, q=P)
+                tile_c = sorted_pool.tile(
+                    [P, SORTED_TILES * K_PASS * CHUNK_ROUNDS[c]], BF16, name="w_sorted"
+                )
+                flat = tile_c[:].bitcast(F32)
                 nc.vector.tensor_copy(
-                    out=w_sorted[c],
-                    in_=w_words[c][:, SORTED_TILE, :].rearrange("p (j q u) -> p j u q", u=2, q=P),
+                    out=flat.rearrange("p (j u q) -> p j u q", u=2, q=P),
+                    in_=w_flat[c][:, FIRST_SORTED_TILE * WORDS_PASS * CHUNK_ROUNDS[c] :].rearrange(
+                        "p (j q u) -> p j u q", u=2, q=P
+                    ),
+                )
+                w_sorted[c] = flat.rearrange(
+                    "p (a j u q) -> p a j u q", a=SORTED_TILES, u=2, q=P
+                )
+
+            def measure_distance(c):
+                spare = grouped.tile([P, WORDS_PASS * CHUNK_ROUNDS[c]], BF16, name="spare", bufs=1)
+                nc.scalar.activation(
+                    out=spare[:],
+                    in_=x_words[c][:, VECTOR_TESTS, :],
+                    func=ACT.Abs,
+                    bias=-PAD_WORD,
+                    accum_out=distance[:, c : c + 1],
                 )
 
             def flip_rows(columns):
@@ -179,7 +203,7 @@ def tile_linearnnencoder_k_kernel(tc, x, W, b, out):
                         nc.vector.tensor_copy(out=ident16[:], in_=ident[:])
                     nc.vector.scalar_tensor_tensor(
                         out=differs[:],
-                        in0=x_words[c][:, :, here],
+                        in0=x_words[c][:, 0:VECTOR_TESTS, here],
                         scalar=PAD_WORD,
                         in1=differs[:],
                         op0=ALU.not_equal,
@@ -191,17 +215,25 @@ def tile_linearnnencoder_k_kernel(tc, x, W, b, out):
                         lambda a, u: x_words[c][:, a, WORDS_PASS * j + u : WORDS_PASS * (j + 1) : 2]
                     )
                     w_banks = flip_rows(
-                        lambda a, u: w_sorted[c][:, j, u, :]
-                        if a == SORTED_TILE and c in w_sorted
+                        lambda a, u: w_sorted[c][:, a - FIRST_SORTED_TILE, j, u, :]
+                        if a >= FIRST_SORTED_TILE and c in w_sorted
                         else w_words[c][:, a, WORDS_PASS * j + u : WORDS_PASS * (j + 1) : 2]
                     )
                     x_rows4 = gather_words(x_banks, "x")
                     w_rows4 = gather_words(w_banks, "w")
+                    if j == 0:
+                        measure_distance(c)
                     if r >= PASS_LAG:
                         multiply_round(r - PASS_LAG)
                     if r == ROUNDS - 1:
                         nc.vector.tensor_reduce(
-                            out=valid_col[:], in_=differs[:], axis=AX.X, op=ALU.max
+                            out=valid_col[:, 0:VECTOR_TESTS], in_=differs[:], axis=AX.X, op=ALU.max
+                        )
+                        nc.vector.tensor_reduce(
+                            out=distance_all[:], in_=distance[:], axis=AX.X, op=ALU.max
+                        )
+                        nc.vector.tensor_single_scalar(
+                            out=valid_col[:, VECTOR_TESTS:], in_=distance_all[:], scalar=0.0, op=ALU.is_gt
                         )
                     split = 4 * P * EARLY_TILES
                     quantised.append(
@@ -252,7 +284,7 @@ def tile_linearnnencoder_k_kernel(tc, x, W, b, out):
                 multiply(quantised[r], r, m, s0, s1)
 
         tail = ctx.enter_context(tc.tile_pool(name="tail", bufs=2))
-        valid = const.tile([P, SAMPLES, TOKENS], F32, name="valid")
+        valid = tail.tile([P, SAMPLES, TOKENS], F32, name="valid", bufs=1)
         nc.scalar.copy(out=valid[:].rearrange("p s t -> p (s t)"), in_=valid_bank[:])
         n_valid = const.tile([P, SAMPLES], F32, name="n_valid")
         nc.vector.tensor_reduce(out=n_valid[:], in_=valid[:], axis=AX.X, op=ALU.add)
@@ -263,7 +295,7 @@ def tile_linearnnencoder_k_kernel(tc, x, W, b, out):
         )
         n_inverse = const.tile([P, 2, SAMPLES], F32, name="n_inverse")
         nc.vector.reciprocal(out=n_inverse[:], in_=n_floor[:])
-        weight = const.tile([P, 2, SAMPLES, TOKENS], F32, name="weight")
+        weight = tail.tile([P, 2, SAMPLES, TOKENS], F32, name="weight", bufs=1)
         for g in range(2):
             nc.vector.tensor_tensor(
                 out=weight[:, g],

@@ -20,23 +20,24 @@ K_PASS = 4 * P
 WORDS_PASS = K_PASS // 2
 ROUNDS = D // K_PASS
 
-CHUNK_ROUNDS = [1] * 8 + [2] * 12
-CHUNKS_AHEAD = 4
+SWEEP_TILES = 2
+LATE_TILES = ROW_TILES - SWEEP_TILES
 
-FIRST_SORTED_TILE = 1
-SORTED_TILES = 4 - FIRST_SORTED_TILE
-FIRST_SORTED = 8
+CHUNK_ROUNDS = [1] * 4 + [2] * 14
+UNIT = 4
+UNITS = ROUNDS // UNIT
+LOADS_AHEAD = 4
 
 VECTOR_TESTS = 3
 
 PASS_LAG = 3
 
-EARLY_TILES = 2
+LAST = ROW_TILES - 1
 LAST_GROUPS = [8, 8]
-FLIP_BANKS = 8 - EARLY_TILES
-FILL_PASSES = 12
+FILL_PASSES = 20
 
 SETTLED_ROUND = 6
+FIRST_SORT_ROUND = ROUNDS - 2
 
 PAD_WORD = -(1.0 + 49024.0 / 8388608.0)
 SQRT_FLOOR = 2.0 ** -100
@@ -57,8 +58,11 @@ def tile_linearnnencoder_k_kernel(tc, x, W, b, out):
         ctx.enter_context(tc.manual_schedule())
         const = ctx.enter_context(tc.tile_pool(name="const", bufs=1))
         packed = ctx.enter_context(tc.tile_pool(name="packed", bufs=ROUNDS))
+        natural = ctx.enter_context(tc.tile_pool(name="natural", bufs=LOADS_AHEAD))
+        sorted_pool = ctx.enter_context(tc.tile_pool(name="sorted", bufs=2))
+        late_grouped = ctx.enter_context(tc.tile_pool(name="late_grouped", bufs=3))
         acc_pool = ctx.enter_context(tc.psum_pool(name="acc", bufs=1))
-        flip_pool = ctx.enter_context(tc.psum_pool(name="flip", bufs=FLIP_BANKS))
+        flip_pool = ctx.enter_context(tc.psum_pool(name="flip", bufs=8 - LAST))
 
         ident = const.tile([P, P], F32, name="ident")
         b_rows = const.tile([P, P], BF16, name="b_rows")
@@ -70,67 +74,100 @@ def tile_linearnnencoder_k_kernel(tc, x, W, b, out):
         distance_all = const.tile([P, 1], F32, name="distance_all")
         valid_col = const.tile([P, ROW_TILES], BF16, name="valid_col")
         ident16 = const.tile([P, P], BF16, name="ident16")
+        in_sample = const.tile([P, P // TOKENS], BF16, name="in_sample")
         bias_col = const.tile([P, ROW_TILES], F32, name="bias_col")
-        acc = [acc_pool.tile([P, ROWS], F32, name="acc%d" % m) for m in range(EARLY_TILES)]
+        acc = [acc_pool.tile([P, ROWS], F32, name="acc%d" % m) for m in range(LAST)]
 
         last_banks = {}
+        x_codes = []
+        early_codes = []
+        late_codes = []
 
-        def sums_of(m, s0, s1):
-            if m == ROW_TILES - 1:
-                return last_banks[s0][:]
-            return acc[m][:, TOKENS * s0 : TOKENS * s1]
-
-        def multiply(operands, r, m, s0=0, s1=SAMPLES):
-            x_codes, x_scales = operands[0]
-            w_codes, w_scales = operands[1 + m // EARLY_TILES]
-            w_cols = slice(P * (m % EARLY_TILES), P * (m % EARLY_TILES + 1))
+        def multiply(r, m, s0=0, s1=SAMPLES):
+            if m < SWEEP_TILES:
+                (w_codes, w_scales), w0 = early_codes[r], P * m
+            else:
+                (w_codes, w_scales), w0 = late_codes[r // 2], P * (LATE_TILES * (r % 2) + m - SWEEP_TILES)
+            w_cols = slice(w0, w0 + P)
             tokens = slice(TOKENS * s0, TOKENS * s1)
             nc.tensor.matmul_mx(
-                out=sums_of(m, s0, s1),
+                out=last_banks[s0][:] if m == LAST else acc[m][:],
                 lhsT=w_codes[:, w_cols].bitcast(FP8X4),
                 lhsT_scale=w_scales[:, w_cols],
-                rhs=x_codes[:, tokens].bitcast(FP8X4),
-                rhs_scale=x_scales[:, tokens],
+                rhs=x_codes[r][0][:, tokens].bitcast(FP8X4),
+                rhs_scale=x_codes[r][1][:, tokens],
                 start=(r == 0),
                 stop=(r == ROUNDS - 1),
             )
 
-        quantised = []
+        x_words = {}
+        w_words = {}
+        late_words = {}
 
-        def multiply_round(r):
-            for m in range(EARLY_TILES):
-                multiply(quantised[r], r, m)
+        def words_of(nat):
+            return nat[:].rearrange("p a k -> p (a k)").bitcast(F32)
 
-        with ExitStack() as streaming:
-            natural = streaming.enter_context(tc.tile_pool(name="natural", bufs=CHUNKS_AHEAD))
-            sorted_pool = streaming.enter_context(tc.tile_pool(name="sorted", bufs=2))
-            grouped = streaming.enter_context(tc.tile_pool(name="grouped", bufs=3))
+        def load_chunk(c, w_natural):
+            k0, width = K_PASS * first_round[c], K_PASS * CHUNK_ROUNDS[c]
+            x_nat = natural.tile([P, ROW_TILES, width], BF16, name="x_nat", tag="nat")
+            w_nat = w_natural.tile([P, SWEEP_TILES, width], BF16, name="w_nat")
+            step = ROW_TILES // 2 if c == 0 else ROW_TILES
+            for nat, rows, tiles in ((x_nat, x_rows, ROW_TILES), (w_nat, w_rows, SWEEP_TILES)):
+                for a in range(0, tiles, step):
+                    a1 = min(a + step, tiles)
+                    nc.sync.dma_start(out=nat[:, a:a1, :], in_=rows[:, a:a1, k0 : k0 + width])
+            x_words[c] = words_of(x_nat).rearrange("p (a w) -> p a w", a=ROW_TILES)
+            w_words[c] = words_of(w_nat).rearrange("p (a w) -> p a w", a=SWEEP_TILES)
 
-            x_words = {}
-            w_words = {}
-            w_flat = {}
-            w_sorted = {}
+        def load_unit(g):
+            k0, width = K_PASS * UNIT * g, K_PASS * UNIT
+            nat = natural.tile([P, LATE_TILES, width], BF16, name="late_nat", tag="nat")
+            nc.sync.dma_start(out=nat[:], in_=w_rows[:, SWEEP_TILES:, k0 : k0 + width])
+            late_words[g] = words_of(nat)
 
-            def as_words(nat):
-                flat = nat[:].rearrange("p a k -> p (a k)").bitcast(F32)
-                return flat.rearrange("p (a w) -> p a w", a=ROW_TILES)
+        def load_ahead(i, w_natural=None):
+            i += LOADS_AHEAD
+            if i < n_chunks:
+                load_chunk(i, w_natural)
+            elif i < n_chunks + UNITS:
+                load_unit(i - n_chunks)
 
-            def load_chunk(c):
-                k0, width = K_PASS * first_round[c], K_PASS * CHUNK_ROUNDS[c]
-                x_nat = natural.tile([P, ROW_TILES, width], BF16, name="x_nat")
-                w_nat = natural.tile([P, ROW_TILES, width], BF16, name="w_nat")
-                step = ROW_TILES // 2 if c == 0 else ROW_TILES
-                for nat, rows in ((x_nat, x_rows), (w_nat, w_rows)):
-                    for a in range(0, ROW_TILES, step):
-                        nc.sync.dma_start(
-                            out=nat[:, a : a + step, :], in_=rows[:, a : a + step, k0 : k0 + width]
-                        )
-                x_words[c] = as_words(x_nat)
-                w_words[c] = as_words(w_nat)
-                w_flat[c] = w_nat[:].rearrange("p a k -> p (a k)").bitcast(F32)
+        def flip_rows(columns):
+            bank = flip_pool.tile([P, 2, 2, P], F32, name="flip")
+            for i in range(2):
+                for u in range(2):
+                    nc.tensor.transpose(bank[:, i, u, :], columns(i, u), ident[:])
+            return bank
 
-            for c in range(CHUNKS_AHEAD):
-                load_chunk(c)
+        def gather_words(bank, rows4):
+            nc.scalar.copy(
+                out=rows4.bitcast(F32).rearrange("p (i r u) -> p i r u", i=2, u=2),
+                in_=bank[:].rearrange("p i u r -> p i r u"),
+            )
+
+        def quantise(rows4, n_rows, bufs, label):
+            codes = packed.tile([P, n_rows], U32, name="%s_codes" % label, align_bytes=64, bufs=bufs)
+            scales = packed.tile([P, n_rows], U8, name="%s_scales" % label, align_bytes=64, bufs=bufs)
+            nc.vector.quantize_mx(out=codes[:].bitcast(FP8X4), scales=scales[:], in_=rows4)
+            return codes, scales
+
+        late_sorted = {}
+
+        def sort_words(g):
+            tile_g = sorted_pool.tile([P, LATE_TILES * UNIT * K_PASS], BF16, name="late_sorted")
+            flat = tile_g[:].bitcast(F32)
+            nc.vector.tensor_copy(
+                out=flat.rearrange("p (j u q) -> p j u q", u=2, q=P),
+                in_=late_words[g].rearrange("p (j q u) -> p j u q", u=2, q=P),
+            )
+            late_sorted[g] = flat.rearrange("p (i j u q) -> p i j u q", i=LATE_TILES, u=2, q=P)
+
+        with ExitStack() as sweep:
+            w_natural = sweep.enter_context(tc.tile_pool(name="w_natural", bufs=LOADS_AHEAD))
+            grouped = sweep.enter_context(tc.tile_pool(name="grouped", bufs=3))
+
+            for c in range(LOADS_AHEAD):
+                load_chunk(c, w_natural)
 
             make_identity(nc, ident[:])
             nc.vector.memset(one[:], 1.0)
@@ -138,21 +175,6 @@ def tile_linearnnencoder_k_kernel(tc, x, W, b, out):
             nc.vector.memset(differs[:], 0.0)
             nc.vector.memset(b_rows[:], 0.0)
             nc.scalar.dma_start(out=b_rows[0:ROW_TILES, :], in_=b.rearrange("(m o) -> m o", o=P))
-
-            def sort_words(c):
-                tile_c = sorted_pool.tile(
-                    [P, SORTED_TILES * K_PASS * CHUNK_ROUNDS[c]], BF16, name="w_sorted"
-                )
-                flat = tile_c[:].bitcast(F32)
-                nc.vector.tensor_copy(
-                    out=flat.rearrange("p (j u q) -> p j u q", u=2, q=P),
-                    in_=w_flat[c][:, FIRST_SORTED_TILE * WORDS_PASS * CHUNK_ROUNDS[c] :].rearrange(
-                        "p (j q u) -> p j u q", u=2, q=P
-                    ),
-                )
-                w_sorted[c] = flat.rearrange(
-                    "p (a j u q) -> p a j u q", a=SORTED_TILES, u=2, q=P
-                )
 
             def measure_distance(c):
                 spare = grouped.tile([P, WORDS_PASS * CHUNK_ROUNDS[c]], BF16, name="spare", bufs=1)
@@ -164,67 +186,44 @@ def tile_linearnnencoder_k_kernel(tc, x, W, b, out):
                     accum_out=distance[:, c : c + 1],
                 )
 
-            def flip_rows(columns):
-                banks = []
-                for half in range(2):
-                    bank = flip_pool.tile([P, 2, 2, P], F32, name="flip")
-                    for i in range(2):
-                        for u in range(2):
-                            nc.tensor.transpose(bank[:, i, u, :], columns(2 * half + i, u), ident[:])
-                    banks.append(bank)
-                return banks
-
-            def gather_words(banks, label):
-                rows4 = grouped.tile([P, 4 * ROWS], BF16, name="%s_rows4" % label, align_bytes=64)
-                by_row = rows4[:].bitcast(F32).rearrange("p (a r u) -> p a r u", a=ROW_TILES, u=2)
-                for half in range(2):
-                    nc.scalar.copy(
-                        out=by_row[:, 2 * half : 2 * half + 2, :, :],
-                        in_=banks[half][:].rearrange("p i u r -> p i r u"),
-                    )
-                return rows4
-
-            def quantise(rows4, n_rows, bufs, label):
-                codes = packed.tile(
-                    [P, n_rows], U32, name="%s_codes" % label, align_bytes=64, bufs=bufs
-                )
-                scales = packed.tile(
-                    [P, n_rows], U8, name="%s_scales" % label, align_bytes=64, bufs=bufs
-                )
-                nc.vector.quantize_mx(out=codes[:].bitcast(FP8X4), scales=scales[:], in_=rows4)
-                return codes, scales
-
             r = 0
             for c in range(n_chunks):
                 for j in range(CHUNK_ROUNDS[c]):
-                    here = slice(WORDS_PASS * j, WORDS_PASS * (j + 1))
+                    w0, w1 = WORDS_PASS * j, WORDS_PASS * (j + 1)
                     if r == SETTLED_ROUND:
                         nc.vector.tensor_copy(out=b_rows32[:], in_=b_rows[:])
                         nc.vector.tensor_copy(out=ident16[:], in_=ident[:])
+                        nc.vector.tensor_reduce(
+                            out=in_sample[:],
+                            in_=ident[:].rearrange("p (s t) -> p s t", t=TOKENS),
+                            axis=AX.X,
+                            op=ALU.max,
+                        )
                     nc.vector.scalar_tensor_tensor(
                         out=differs[:],
-                        in0=x_words[c][:, 0:VECTOR_TESTS, here],
+                        in0=x_words[c][:, 0:VECTOR_TESTS, w0:w1],
                         scalar=PAD_WORD,
                         in1=differs[:],
                         op0=ALU.not_equal,
                         op1=ALU.max,
                     )
-                    if j == 0 and FIRST_SORTED <= c + 1 < n_chunks:
-                        sort_words(c + 1)
-                    x_banks = flip_rows(
-                        lambda a, u: x_words[c][:, a, WORDS_PASS * j + u : WORDS_PASS * (j + 1) : 2]
-                    )
-                    w_banks = flip_rows(
-                        lambda a, u: w_sorted[c][:, a - FIRST_SORTED_TILE, j, u, :]
-                        if a >= FIRST_SORTED_TILE and c in w_sorted
-                        else w_words[c][:, a, WORDS_PASS * j + u : WORDS_PASS * (j + 1) : 2]
-                    )
-                    x_rows4 = gather_words(x_banks, "x")
-                    w_rows4 = gather_words(w_banks, "w")
+                    x_banks = [
+                        flip_rows(lambda i, u: x_words[c][:, 2 * half + i, w0 + u : w1 : 2])
+                        for half in range(2)
+                    ]
+                    w_bank = flip_rows(lambda i, u: w_words[c][:, i, w0 + u : w1 : 2])
+                    x_rows4 = grouped.tile([P, 4 * ROWS], BF16, name="x_rows4", align_bytes=64)
+                    w_rows4 = grouped.tile([P, 8 * P], BF16, name="w_rows4", align_bytes=64)
+                    for half in range(2):
+                        gather_words(x_banks[half], x_rows4[:, 8 * P * half : 8 * P * (half + 1)])
+                    gather_words(w_bank, w_rows4[:])
                     if j == 0:
                         measure_distance(c)
                     if r >= PASS_LAG:
-                        multiply_round(r - PASS_LAG)
+                        for m in range(SWEEP_TILES):
+                            multiply(r - PASS_LAG, m)
+                    if r == FIRST_SORT_ROUND:
+                        sort_words(0)
                     if r == ROUNDS - 1:
                         nc.vector.tensor_reduce(
                             out=valid_col[:, 0:VECTOR_TESTS], in_=differs[:], axis=AX.X, op=ALU.max
@@ -235,157 +234,171 @@ def tile_linearnnencoder_k_kernel(tc, x, W, b, out):
                         nc.vector.tensor_single_scalar(
                             out=valid_col[:, VECTOR_TESTS:], in_=distance_all[:], scalar=0.0, op=ALU.is_gt
                         )
-                    split = 4 * P * EARLY_TILES
-                    quantised.append(
-                        [
-                            quantise(x_rows4[:], ROWS, ROUNDS, "x"),
-                            quantise(w_rows4[:, :split], P * EARLY_TILES, PASS_LAG + 2, "w_early"),
-                            quantise(
-                                w_rows4[:, split:], P * (ROW_TILES - EARLY_TILES), ROUNDS, "w_late"
-                            ),
-                        ]
-                    )
+                    x_codes.append(quantise(x_rows4[:], ROWS, ROUNDS, "x"))
+                    early_codes.append(quantise(w_rows4[:], SWEEP_TILES * P, PASS_LAG + 2, "w_early"))
                     r += 1
-                if c + CHUNKS_AHEAD < n_chunks:
-                    load_chunk(c + CHUNKS_AHEAD)
-
-        for late_round in range(ROUNDS - PASS_LAG, ROUNDS - 1):
-            multiply_round(late_round)
-
-        b_flip = flip_pool.tile([P, P], F32, name="b_flip", tag="flip")
-        nc.tensor.transpose(b_flip[:], b_rows32[:], ident[:])
-        nc.scalar.copy(out=bias_col[:], in_=b_flip[:, 0:ROW_TILES])
-        valid_bank = flip_pool.tile([P, ROWS], F32, name="valid_bank", tag="flip")
-        for a in range(ROW_TILES):
-            nc.tensor.matmul(
-                out=valid_bank[:, P * a : P * (a + 1)],
-                lhsT=valid_col[:, a : a + 1].to_broadcast([P, P]),
-                rhs=ident16[:],
-                start=True,
-                stop=True,
-            )
-
-        units = [(m, 0, SAMPLES) for m in range(ROW_TILES - 1)]
-        for g in range(len(LAST_GROUPS)):
-            units.append((ROW_TILES - 1, sum(LAST_GROUPS[:g]), sum(LAST_GROUPS[: g + 1])))
-        for m in range(EARLY_TILES, ROW_TILES - 1):
-            acc.append(flip_pool.tile([P, ROWS], F32, name="acc%d" % m, tag="flip"))
-        for m, s0, s1 in units[ROW_TILES - 1 :]:
-            last_banks[s0] = flip_pool.tile(
-                [P, TOKENS * (s1 - s0)], F32, name="last%d" % s0, tag="flip"
-            )
-        for r in range(FILL_PASSES):
-            multiply(quantised[r], r, EARLY_TILES)
-        multiply_round(ROUNDS - 1)
-        for r in range(FILL_PASSES, ROUNDS):
-            multiply(quantised[r], r, EARLY_TILES)
-        for m, s0, s1 in units[EARLY_TILES + 1 :]:
-            for r in range(ROUNDS):
-                multiply(quantised[r], r, m, s0, s1)
+                load_ahead(c, w_natural)
 
         tail = ctx.enter_context(tc.tile_pool(name="tail", bufs=2))
-        valid = tail.tile([P, SAMPLES, TOKENS], F32, name="valid", bufs=1)
-        nc.scalar.copy(out=valid[:].rearrange("p s t -> p (s t)"), in_=valid_bank[:])
-        n_valid = const.tile([P, SAMPLES], F32, name="n_valid")
-        nc.vector.tensor_reduce(out=n_valid[:], in_=valid[:], axis=AX.X, op=ALU.add)
-        n_floor = const.tile([P, 2, SAMPLES], F32, name="n_floor")
-        nc.vector.tensor_scalar_max(out=n_floor[:, 0, :], in0=n_valid[:], scalar1=1.0)
-        nc.vector.tensor_scalar(
-            out=n_floor[:, 1, :], in0=n_valid[:], scalar1=-1.0, scalar2=1.0, op0=ALU.add, op1=ALU.max
-        )
-        n_inverse = const.tile([P, 2, SAMPLES], F32, name="n_inverse")
-        nc.vector.reciprocal(out=n_inverse[:], in_=n_floor[:])
-        weight = tail.tile([P, 2, SAMPLES, TOKENS], F32, name="weight", bufs=1)
-        for g in range(2):
-            nc.vector.tensor_tensor(
-                out=weight[:, g],
-                in0=valid[:],
-                in1=n_inverse[:, g, :].unsqueeze(2).to_broadcast([P, SAMPLES, TOKENS]),
-                op=ALU.mult,
-            )
-
+        units = [(m, 0, SAMPLES) for m in range(LAST)]
+        for g in range(len(LAST_GROUPS)):
+            units.append((LAST, sum(LAST_GROUPS[:g]), sum(LAST_GROUPS[: g + 1])))
         stats = const.tile([P, SAMPLES, 2, ROW_TILES], F32, name="stats")
         variance = const.tile([P, SAMPLES, ROW_TILES], F32, name="variance")
-        y = []
+        weight = tail.tile([P, 2, SAMPLES, TOKENS], F32, name="weight", bufs=1)
+        y = {}
+        share = {}
+        away = {}
+        squares = {}
+        square_share = {}
+        banks = {}
 
-        def gelu(unit):
-            m, s0, s1 = unit
-            y_u = tail.tile([P, s1 - s0, TOKENS], F32, name="y", bufs=len(units))
+        def spread_flags():
+            banks["small"] = flip_pool.tile([P, P + SAMPLES], F32, name="small", tag="flip")
+            banks["valid"] = flip_pool.tile([P, ROWS], F32, name="valid", tag="flip")
+            nc.tensor.transpose(banks["small"][:, 0:P], b_rows32[:], ident[:])
+            per_tile = P // TOKENS
+            for a in range(ROW_TILES):
+                flags = valid_col[:, a : a + 1].to_broadcast([P, P])
+                for o_cols, rhs in (
+                    (banks["valid"][:, P * a : P * (a + 1)], ident16),
+                    (banks["small"][:, P + per_tile * a : P + per_tile * (a + 1)], in_sample),
+                ):
+                    nc.tensor.matmul(out=o_cols, lhsT=flags, rhs=rhs[:], start=True, stop=True)
+
+        def find_bias():
+            nc.scalar.copy(out=bias_col[:], in_=banks["small"][:, 0:ROW_TILES])
+
+        def find_weights():
+            count = banks["small"][:, P : P + SAMPLES]
+            n_floor = const.tile([P, 2, SAMPLES], F32, name="n_floor")
+            nc.vector.tensor_scalar_max(out=n_floor[:, 0, :], in0=count, scalar1=1.0)
+            nc.vector.tensor_scalar(
+                out=n_floor[:, 1, :], in0=count, scalar1=-1.0, scalar2=1.0, op0=ALU.add, op1=ALU.max
+            )
+            n_inverse = const.tile([P, 2, SAMPLES], F32, name="n_inverse")
+            nc.vector.reciprocal(out=n_inverse[:], in_=n_floor[:])
+            for g in range(2):
+                nc.vector.tensor_tensor(
+                    out=weight[:, g],
+                    in0=banks["valid"][:].rearrange("p (s t) -> p s t", t=TOKENS),
+                    in1=n_inverse[:, g, :].unsqueeze(2).to_broadcast([P, SAMPLES, TOKENS]),
+                    op=ALU.mult,
+                )
+
+        def gelu(i):
+            m, s0, s1 = units[i]
+            y[i] = tail.tile([P, s1 - s0, TOKENS], F32, name="y", bufs=len(units))
             nc.scalar.activation(
-                out=y_u[:].rearrange("p s t -> p (s t)"),
-                in_=sums_of(m, s0, s1),
+                out=y[i][:].rearrange("p s t -> p (s t)"),
+                in_=last_banks[s0][:] if m == LAST else acc[m][:],
                 func=ACT.Gelu,
                 bias=bias_col[:, m : m + 1],
             )
-            y.append(y_u)
-
-        away = {}
-        squares = {}
 
         def find_share(i):
-            m, s0, s1 = units[i]
-            share = tail.tile([P, s1 - s0, TOKENS], F32, name="share")
-            nc.vector.tensor_tensor(out=share[:], in0=y[i][:], in1=weight[:, 0, s0:s1, :], op=ALU.mult)
-            return share
+            share[i] = tail.tile([P, SAMPLES, TOKENS], F32, name="share")
+            nc.vector.tensor_tensor(out=share[i][:], in0=y[i][:], in1=weight[:, 0], op=ALU.mult)
 
-        def find_mean(i, share):
-            m, s0, s1 = units[i]
-            nc.vector.tensor_reduce(out=stats[:, s0:s1, 1, m], in_=share[:], axis=AX.X, op=ALU.add)
+        def find_mean(i):
+            nc.vector.tensor_reduce(out=stats[:, :, 1, i], in_=share[i][:], axis=AX.X, op=ALU.add)
 
         def find_away(i):
-            m, s0, s1 = units[i]
-            shape = [P, s1 - s0, TOKENS]
+            shape = [P, SAMPLES, TOKENS]
             away[i] = tail.tile(shape, F32, name="away")
             nc.vector.tensor_tensor(
                 out=away[i][:],
                 in0=y[i][:],
-                in1=stats[:, s0:s1, 1, m].unsqueeze(2).to_broadcast(shape),
+                in1=stats[:, :, 1, i].unsqueeze(2).to_broadcast(shape),
                 op=ALU.subtract,
             )
 
-        def square_on_scalar(i):
-            m, s0, s1 = units[i]
-            squares[i] = tail.tile([P, s1 - s0, TOKENS], F32, name="squares")
+        def square(i):
+            squares[i] = tail.tile([P, SAMPLES, TOKENS], F32, name="squares")
             nc.scalar.activation(out=squares[i][:], in_=away[i][:], func=ACT.Square)
 
         def find_square_share(i):
-            m, s0, s1 = units[i]
-            square_share = tail.tile([P, s1 - s0, TOKENS], F32, name="square_share")
+            square_share[i] = tail.tile([P, SAMPLES, TOKENS], F32, name="square_share")
             nc.vector.tensor_tensor(
-                out=square_share[:], in0=squares[i][:], in1=weight[:, 1, s0:s1, :], op=ALU.mult
+                out=square_share[i][:], in0=squares[i][:], in1=weight[:, 1], op=ALU.mult
             )
-            return square_share
 
-        def find_variance(i, square_share):
-            m, s0, s1 = units[i]
+        def find_variance(i):
             nc.vector.tensor_reduce(
-                out=variance[:, s0:s1, m], in_=square_share[:], axis=AX.X, op=ALU.add
+                out=variance[:, :, i], in_=square_share[i][:], axis=AX.X, op=ALU.add
             )
 
-        early = list(range(EARLY_TILES))
-        for i in early:
-            gelu(units[i])
-        shares = [find_share(i) for i in early]
-        for i in early:
-            find_mean(i, shares[i])
-        for i in early:
-            find_away(i)
-            square_on_scalar(i)
-        gelu(units[EARLY_TILES])
-        square_shares = [find_square_share(i) for i in early]
-        for i in early:
-            find_variance(i, square_shares[i])
-        for i in range(EARLY_TILES, ROW_TILES - 1):
-            find_mean(i, find_share(i))
-            find_away(i)
-            square_on_scalar(i)
-            gelu(units[i + 1])
-            find_variance(i, find_square_share(i))
+        beside = [
+            [find_bias],
+            [find_weights, lambda: gelu(0), lambda: gelu(1)],
+            [lambda: find_share(0), lambda: find_share(1)],
+            [lambda: find_mean(0)],
+            [lambda: find_mean(1)],
+            [lambda: find_away(0)],
+            [lambda: find_away(1), lambda: square(0)],
+            [lambda: square(1)],
+        ]
 
-        for i in range(ROW_TILES - 1, len(units)):
+        for g in range(UNITS):
+            late_banks = [
+                flip_rows(lambda i, u: late_sorted[g][:, i, j, u, :]) for j in range(UNIT)
+            ]
+            late_rows4 = []
+            for j in range(UNIT):
+                if j % 2 == 0:
+                    late_rows4.append(
+                        late_grouped.tile([P, 16 * P], BF16, name="late_rows4", align_bytes=64)
+                    )
+                half = late_rows4[-1][:, 8 * P * (j % 2) : 8 * P * (j % 2 + 1)]
+                gather_words(late_banks[j], half)
+            if g == 0:
+                spread_flags()
+                for r in range(ROUNDS - PASS_LAG, ROUNDS):
+                    for m in range(SWEEP_TILES):
+                        multiply(r, m)
+            else:
+                for r in range(UNIT * (g - 1), UNIT * g):
+                    multiply(r, SWEEP_TILES)
+            if g + 1 < UNITS:
+                sort_words(g + 1)
+                load_ahead(n_chunks + g)
+            for rows4 in late_rows4:
+                late_codes.append(quantise(rows4[:], 4 * P, ROUNDS // 2, "w_late"))
+            for step in beside[g]:
+                step()
+
+        for i in range(LAST, len(units)):
+            m, s0, s1 = units[i]
+            last_banks[s0] = acc_pool.tile(
+                [P, TOKENS * (s1 - s0)], F32, name="last%d" % s0, tag="acc%d" % (i - LAST)
+            )
+        for r in range(FILL_PASSES):
+            multiply(r, *units[LAST])
+        for r in range(ROUNDS - UNIT, ROUNDS):
+            multiply(r, SWEEP_TILES)
+        for r in range(FILL_PASSES, ROUNDS):
+            multiply(r, *units[LAST])
+        for unit in units[LAST + 1 :]:
+            for r in range(ROUNDS):
+                multiply(r, *unit)
+
+        for i in range(SWEEP_TILES):
+            find_square_share(i)
+        for i in range(SWEEP_TILES):
+            find_variance(i)
+        gelu(SWEEP_TILES)
+        find_share(SWEEP_TILES)
+        find_mean(SWEEP_TILES)
+        find_away(SWEEP_TILES)
+        square(SWEEP_TILES)
+        gelu(LAST)
+        find_square_share(SWEEP_TILES)
+        find_variance(SWEEP_TILES)
+
+        for i in range(LAST, len(units)):
             m, s0, s1 = units[i]
             if i + 1 < len(units):
-                gelu(units[i + 1])
+                gelu(i + 1)
             spare = tail.tile([P, s1 - s0, TOKENS], F32, name="spare")
             away_share = tail.tile([P, s1 - s0, TOKENS], F32, name="away_share")
             for s in range(s0, s1):

@@ -27,6 +27,8 @@ CHUNK_ROUNDS = [1] * 4 + [2] * 14
 UNIT = 4
 UNITS = ROUNDS // UNIT
 LOADS_AHEAD = 4
+SORT_BEHIND_CHUNK = [9, 11, 13, 15]
+SORT_BEHIND_UNIT = [0, 2, 3, 5]
 
 VECTOR_TESTS = 3
 
@@ -37,7 +39,6 @@ LAST_GROUPS = [8, 8]
 FILL_PASSES = 20
 
 SETTLED_ROUND = 6
-FIRST_SORT_ROUND = ROUNDS - 2
 
 PAD_WORD = -(1.0 + 49024.0 / 8388608.0)
 SQRT_FLOOR = 2.0 ** -100
@@ -59,8 +60,8 @@ def tile_linearnnencoder_k_kernel(tc, x, W, b, out):
         const = ctx.enter_context(tc.tile_pool(name="const", bufs=1))
         packed = ctx.enter_context(tc.tile_pool(name="packed", bufs=ROUNDS))
         natural = ctx.enter_context(tc.tile_pool(name="natural", bufs=LOADS_AHEAD))
-        sorted_pool = ctx.enter_context(tc.tile_pool(name="sorted", bufs=2))
-        late_grouped = ctx.enter_context(tc.tile_pool(name="late_grouped", bufs=3))
+        sorted_pool = ctx.enter_context(tc.tile_pool(name="sorted", bufs=len(SORT_BEHIND_CHUNK)))
+        late_grouped = ctx.enter_context(tc.tile_pool(name="late_grouped", bufs=2))
         acc_pool = ctx.enter_context(tc.psum_pool(name="acc", bufs=1))
         flip_pool = ctx.enter_context(tc.psum_pool(name="flip", bufs=8 - LAST))
 
@@ -125,12 +126,23 @@ def tile_linearnnencoder_k_kernel(tc, x, W, b, out):
             nc.sync.dma_start(out=nat[:], in_=w_rows[:, SWEEP_TILES:, k0 : k0 + width])
             late_words[g] = words_of(nat)
 
-        def load_ahead(i, w_natural=None):
-            i += LOADS_AHEAD
-            if i < n_chunks:
-                load_chunk(i, w_natural)
-            elif i < n_chunks + UNITS:
-                load_unit(i - n_chunks)
+        loads = []
+        for c in range(n_chunks):
+            loads.append(c)
+            if c in SORT_BEHIND_CHUNK:
+                loads.append(n_chunks + SORT_BEHIND_CHUNK.index(c))
+        loads += [n_chunks + g for g in range(len(SORT_BEHIND_CHUNK), UNITS)]
+
+        def load_item(i, w_natural):
+            if loads[i] < n_chunks:
+                load_chunk(loads[i], w_natural)
+            else:
+                load_unit(loads[i] - n_chunks)
+
+        def used_up(item, w_natural=None):
+            i = loads.index(item) + LOADS_AHEAD
+            if i < len(loads):
+                load_item(i, w_natural)
 
         def flip_rows(columns):
             bank = flip_pool.tile([P, 2, 2, P], F32, name="flip")
@@ -163,11 +175,11 @@ def tile_linearnnencoder_k_kernel(tc, x, W, b, out):
             late_sorted[g] = flat.rearrange("p (i j u q) -> p i j u q", i=LATE_TILES, u=2, q=P)
 
         with ExitStack() as sweep:
-            w_natural = sweep.enter_context(tc.tile_pool(name="w_natural", bufs=LOADS_AHEAD))
+            w_natural = sweep.enter_context(tc.tile_pool(name="w_natural", bufs=3))
             grouped = sweep.enter_context(tc.tile_pool(name="grouped", bufs=3))
 
-            for c in range(LOADS_AHEAD):
-                load_chunk(c, w_natural)
+            for i in range(LOADS_AHEAD):
+                load_item(i, w_natural)
 
             make_identity(nc, ident[:])
             nc.vector.memset(one[:], 1.0)
@@ -222,8 +234,6 @@ def tile_linearnnencoder_k_kernel(tc, x, W, b, out):
                     if r >= PASS_LAG:
                         for m in range(SWEEP_TILES):
                             multiply(r - PASS_LAG, m)
-                    if r == FIRST_SORT_ROUND:
-                        sort_words(0)
                     if r == ROUNDS - 1:
                         nc.vector.tensor_reduce(
                             out=valid_col[:, 0:VECTOR_TESTS], in_=differs[:], axis=AX.X, op=ALU.max
@@ -237,7 +247,11 @@ def tile_linearnnencoder_k_kernel(tc, x, W, b, out):
                     x_codes.append(quantise(x_rows4[:], ROWS, ROUNDS, "x"))
                     early_codes.append(quantise(w_rows4[:], SWEEP_TILES * P, PASS_LAG + 2, "w_early"))
                     r += 1
-                load_ahead(c, w_natural)
+                used_up(c, w_natural)
+                if c in SORT_BEHIND_CHUNK:
+                    g = SORT_BEHIND_CHUNK.index(c)
+                    sort_words(g)
+                    used_up(n_chunks + g, w_natural)
 
         tail = ctx.enter_context(tc.tile_pool(name="tail", bufs=2))
         units = [(m, 0, SAMPLES) for m in range(LAST)]
@@ -318,7 +332,7 @@ def tile_linearnnencoder_k_kernel(tc, x, W, b, out):
             nc.scalar.activation(out=squares[i][:], in_=away[i][:], func=ACT.Square)
 
         def find_square_share(i):
-            square_share[i] = tail.tile([P, SAMPLES, TOKENS], F32, name="square_share")
+            square_share[i] = tail.tile([P, SAMPLES, TOKENS], F32, name="square_share", tag="share")
             nc.vector.tensor_tensor(
                 out=square_share[i][:], in0=squares[i][:], in1=weight[:, 1], op=ALU.mult
             )
@@ -331,12 +345,12 @@ def tile_linearnnencoder_k_kernel(tc, x, W, b, out):
         beside = [
             [find_bias],
             [find_weights, lambda: gelu(0), lambda: gelu(1)],
+            [],
+            [],
             [lambda: find_share(0), lambda: find_share(1)],
-            [lambda: find_mean(0)],
-            [lambda: find_mean(1)],
-            [lambda: find_away(0)],
-            [lambda: find_away(1), lambda: square(0)],
-            [lambda: square(1)],
+            [],
+            [lambda: find_mean(0), lambda: find_mean(1)],
+            [lambda: find_away(0), lambda: find_away(1)],
         ]
 
         for g in range(UNITS):
@@ -359,11 +373,12 @@ def tile_linearnnencoder_k_kernel(tc, x, W, b, out):
             else:
                 for r in range(UNIT * (g - 1), UNIT * g):
                     multiply(r, SWEEP_TILES)
-            if g + 1 < UNITS:
-                sort_words(g + 1)
-                load_ahead(n_chunks + g)
             for rows4 in late_rows4:
                 late_codes.append(quantise(rows4[:], 4 * P, ROUNDS // 2, "w_late"))
+            if g in SORT_BEHIND_UNIT:
+                later = len(SORT_BEHIND_CHUNK) + SORT_BEHIND_UNIT.index(g)
+                sort_words(later)
+                used_up(n_chunks + later)
             for step in beside[g]:
                 step()
 
@@ -382,6 +397,8 @@ def tile_linearnnencoder_k_kernel(tc, x, W, b, out):
             for r in range(ROUNDS):
                 multiply(r, *unit)
 
+        for i in range(SWEEP_TILES):
+            square(i)
         for i in range(SWEEP_TILES):
             find_square_share(i)
         for i in range(SWEEP_TILES):

@@ -33,6 +33,7 @@ SORT_BEHIND_UNIT = [0, 2, 3, 5]
 VECTOR_TESTS = 3
 
 PASS_LAG = 3
+RUN_BANKS = 4
 
 LAST = ROW_TILES - 1
 LAST_GROUPS = [8, 8]
@@ -198,6 +199,8 @@ def tile_linearnnencoder_k_kernel(tc, x, W, b, out):
                     accum_out=distance[:, c : c + 1],
                 )
 
+            filled = 0
+            multiplied = 0
             r = 0
             for c in range(n_chunks):
                 for j in range(CHUNK_ROUNDS[c]):
@@ -219,21 +222,23 @@ def tile_linearnnencoder_k_kernel(tc, x, W, b, out):
                         op0=ALU.not_equal,
                         op1=ALU.max,
                     )
-                    x_banks = [
-                        flip_rows(lambda i, u: x_words[c][:, 2 * half + i, w0 + u : w1 : 2])
-                        for half in range(2)
-                    ]
-                    w_bank = flip_rows(lambda i, u: w_words[c][:, i, w0 + u : w1 : 2])
                     x_rows4 = grouped.tile([P, 4 * ROWS], BF16, name="x_rows4", align_bytes=64)
                     w_rows4 = grouped.tile([P, 8 * P], BF16, name="w_rows4", align_bytes=64)
-                    for half in range(2):
-                        gather_words(x_banks[half], x_rows4[:, 8 * P * half : 8 * P * (half + 1)])
-                    gather_words(w_bank, w_rows4[:])
+                    for words, a, rows4 in (
+                        (x_words[c], 0, x_rows4[:, : 8 * P]),
+                        (x_words[c], 2, x_rows4[:, 8 * P :]),
+                        (w_words[c], 0, w_rows4[:]),
+                    ):
+                        bank = flip_rows(lambda i, u: words[:, a + i, w0 + u : w1 : 2])
+                        gather_words(bank, rows4)
+                        filled += 1
+                        if filled % RUN_BANKS == 0:
+                            while multiplied <= r - PASS_LAG:
+                                for m in range(SWEEP_TILES):
+                                    multiply(multiplied, m)
+                                multiplied += 1
                     if j == 0:
                         measure_distance(c)
-                    if r >= PASS_LAG:
-                        for m in range(SWEEP_TILES):
-                            multiply(r - PASS_LAG, m)
                     if r == ROUNDS - 1:
                         nc.vector.tensor_reduce(
                             out=valid_col[:, 0:VECTOR_TESTS], in_=differs[:], axis=AX.X, op=ALU.max
@@ -354,27 +359,19 @@ def tile_linearnnencoder_k_kernel(tc, x, W, b, out):
         ]
 
         for g in range(UNITS):
-            late_banks = [
-                flip_rows(lambda i, u: late_sorted[g][:, i, j, u, :]) for j in range(UNIT)
-            ]
-            late_rows4 = []
-            for j in range(UNIT):
-                if j % 2 == 0:
-                    late_rows4.append(
-                        late_grouped.tile([P, 16 * P], BF16, name="late_rows4", align_bytes=64)
-                    )
-                half = late_rows4[-1][:, 8 * P * (j % 2) : 8 * P * (j % 2 + 1)]
-                gather_words(late_banks[j], half)
+            for pair in range(UNIT // 2):
+                rows4 = late_grouped.tile([P, 16 * P], BF16, name="late_rows4", align_bytes=64)
+                for j in range(2 * pair, 2 * pair + 2):
+                    bank = flip_rows(lambda i, u: late_sorted[g][:, i, j, u, :])
+                    gather_words(bank, rows4[:, 8 * P * (j % 2) : 8 * P * (j % 2 + 1)])
+                late_codes.append(quantise(rows4[:], 4 * P, ROUNDS // 2, "w_late"))
             if g == 0:
                 spread_flags()
-                for r in range(ROUNDS - PASS_LAG, ROUNDS):
+                for r in range(multiplied, ROUNDS):
                     for m in range(SWEEP_TILES):
                         multiply(r, m)
-            else:
-                for r in range(UNIT * (g - 1), UNIT * g):
-                    multiply(r, SWEEP_TILES)
-            for rows4 in late_rows4:
-                late_codes.append(quantise(rows4[:], 4 * P, ROUNDS // 2, "w_late"))
+            for r in range(UNIT * max(g - 1, 0), UNIT * g):
+                multiply(r, SWEEP_TILES)
             if g in SORT_BEHIND_UNIT:
                 later = len(SORT_BEHIND_CHUNK) + SORT_BEHIND_UNIT.index(g)
                 sort_words(later)

@@ -13,6 +13,7 @@ ACT = mybir.ActivationFunctionType
 AX = mybir.AxisListType
 
 P = 128
+ALIGN = 256
 SAMPLES, TOKENS, D, O = 16, 32, 16384, 512
 ROWS = SAMPLES * TOKENS
 ROW_TILES = ROWS // P
@@ -66,7 +67,7 @@ def tile_linearnnencoder_k_kernel(tc, x, W, b, out):
         acc_pool = ctx.enter_context(tc.psum_pool(name="acc", bufs=1))
         flip_pool = ctx.enter_context(tc.psum_pool(name="flip", bufs=8 - LAST))
 
-        ident = const.tile([P, P], F32, name="ident")
+        ident = const.tile([P, P], F32, name="ident", align_bytes=ALIGN)
         b_rows = const.tile([P, P], BF16, name="b_rows")
         b_rows32 = const.tile([P, P], F32, name="b_rows32")
         one = const.tile([P, 1], F32, name="one")
@@ -111,8 +112,12 @@ def tile_linearnnencoder_k_kernel(tc, x, W, b, out):
 
         def load_chunk(c, w_natural):
             k0, width = K_PASS * first_round[c], K_PASS * CHUNK_ROUNDS[c]
-            x_nat = natural.tile([P, ROW_TILES, width], BF16, name="x_nat", tag="nat")
-            w_nat = w_natural.tile([P, SWEEP_TILES, width], BF16, name="w_nat")
+            x_nat = natural.tile(
+                [P, ROW_TILES, width], BF16, name="x_nat", tag="nat", align_bytes=ALIGN
+            )
+            w_nat = w_natural.tile(
+                [P, SWEEP_TILES, width], BF16, name="w_nat", align_bytes=ALIGN
+            )
             step = ROW_TILES // 2 if c == 0 else ROW_TILES
             for nat, rows, tiles in ((x_nat, x_rows, ROW_TILES), (w_nat, w_rows, SWEEP_TILES)):
                 for a in range(0, tiles, step):
@@ -123,7 +128,9 @@ def tile_linearnnencoder_k_kernel(tc, x, W, b, out):
 
         def load_unit(g):
             k0, width = K_PASS * UNIT * g, K_PASS * UNIT
-            nat = natural.tile([P, LATE_TILES, width], BF16, name="late_nat", tag="nat")
+            nat = natural.tile(
+                [P, LATE_TILES, width], BF16, name="late_nat", tag="nat", align_bytes=ALIGN
+            )
             nc.sync.dma_start(out=nat[:], in_=w_rows[:, SWEEP_TILES:, k0 : k0 + width])
             late_words[g] = words_of(nat)
 
@@ -159,15 +166,17 @@ def tile_linearnnencoder_k_kernel(tc, x, W, b, out):
             )
 
         def quantise(rows4, n_rows, bufs, label):
-            codes = packed.tile([P, n_rows], U32, name="%s_codes" % label, align_bytes=64, bufs=bufs)
-            scales = packed.tile([P, n_rows], U8, name="%s_scales" % label, align_bytes=64, bufs=bufs)
+            codes = packed.tile([P, n_rows], U32, name="%s_codes" % label, align_bytes=ALIGN, bufs=bufs)
+            scales = packed.tile([P, n_rows], U8, name="%s_scales" % label, align_bytes=ALIGN, bufs=bufs)
             nc.vector.quantize_mx(out=codes[:].bitcast(FP8X4), scales=scales[:], in_=rows4)
             return codes, scales
 
         late_sorted = {}
 
         def sort_words(g):
-            tile_g = sorted_pool.tile([P, LATE_TILES * UNIT * K_PASS], BF16, name="late_sorted")
+            tile_g = sorted_pool.tile(
+                [P, LATE_TILES * UNIT * K_PASS], BF16, name="late_sorted", align_bytes=ALIGN
+            )
             flat = tile_g[:].bitcast(F32)
             nc.vector.tensor_copy(
                 out=flat.rearrange("p (j u q) -> p j u q", u=2, q=P),
@@ -222,8 +231,8 @@ def tile_linearnnencoder_k_kernel(tc, x, W, b, out):
                         op0=ALU.not_equal,
                         op1=ALU.max,
                     )
-                    x_rows4 = grouped.tile([P, 4 * ROWS], BF16, name="x_rows4", align_bytes=64)
-                    w_rows4 = grouped.tile([P, 8 * P], BF16, name="w_rows4", align_bytes=64)
+                    x_rows4 = grouped.tile([P, 4 * ROWS], BF16, name="x_rows4", align_bytes=ALIGN)
+                    w_rows4 = grouped.tile([P, 8 * P], BF16, name="w_rows4", align_bytes=ALIGN)
                     for words, a, rows4 in (
                         (x_words[c], 0, x_rows4[:, : 8 * P]),
                         (x_words[c], 2, x_rows4[:, 8 * P :]),
@@ -360,7 +369,7 @@ def tile_linearnnencoder_k_kernel(tc, x, W, b, out):
 
         for g in range(UNITS):
             for pair in range(UNIT // 2):
-                rows4 = late_grouped.tile([P, 16 * P], BF16, name="late_rows4", align_bytes=64)
+                rows4 = late_grouped.tile([P, 16 * P], BF16, name="late_rows4", align_bytes=ALIGN)
                 for j in range(2 * pair, 2 * pair + 2):
                     bank = flip_rows(lambda i, u: late_sorted[g][:, i, j, u, :])
                     gather_words(bank, rows4[:, 8 * P * (j % 2) : 8 * P * (j % 2 + 1)])

from contextlib import ExitStack

import concourse.mybir as mybir
from concourse.masks import make_identity

F32 = mybir.dt.float32
BF16 = mybir.dt.bfloat16
U32 = mybir.dt.uint32
U8 = mybir.dt.uint8
FP8X4 = mybir.dt.float8_e4m3fn_x4
ALU = mybir.AluOpType
ACT = mybir.ActivationFunctionType
AX = mybir.AxisListType

P = 128
ALIGN = 256
SAMPLES, TOKENS, D, O = 16, 32, 16384, 512
ROWS = SAMPLES * TOKENS
ROW_TILES = ROWS // P
K_PASS = 4 * P
WORDS_PASS = K_PASS // 2
ROUNDS = D // K_PASS

SWEEP_TILES = 2
LATE_TILES = ROW_TILES - SWEEP_TILES

CHUNK_ROUNDS = [1] * 4 + [2] * 14
UNIT = 4
UNITS = ROUNDS // UNIT
LOADS_AHEAD = 4
SORT_BEHIND_CHUNK = [9, 11, 13, 15]
SORT_BEHIND_UNIT = [0, 2, 3, 5]

VECTOR_TESTS = 3

PASS_LAG = 3
RUN_BANKS = 4

LAST = ROW_TILES - 1
LAST_GROUPS = [8, 8]
FILL_PASSES = 20

SETTLED_ROUND = 6

PAD_WORD = -(1.0 + 49024.0 / 8388608.0)
SQRT_FLOOR = 2.0 ** -100

FLOPS = 2 * ROWS * O * D


def tile_linearnnencoder_k_kernel(tc, x, W, b, out):
    nc = tc.nc
    assert sum(CHUNK_ROUNDS) == ROUNDS
    n_chunks = len(CHUNK_ROUNDS)
    first_round = [sum(CHUNK_ROUNDS[:c]) for c in range(n_chunks)]

    x_rows = x.rearrange("s t k -> (s t) k").rearrange("(a p) k -> p a k", p=P)
    w_rows = W.rearrange("(a p) k -> p a k", p=P)

    with ExitStack() as ctx:
        ctx.enter_context(tc.manual_schedule())
        const = ctx.enter_context(tc.tile_pool(name="const", bufs=1))
        packed = ctx.enter_context(tc.tile_pool(name="packed", bufs=ROUNDS))
        natural = ctx.enter_context(tc.tile_pool(name="natural", bufs=LOADS_AHEAD))
        sorted_pool = ctx.enter_context(tc.tile_pool(name="sorted", bufs=len(SORT_BEHIND_CHUNK)))
        late_grouped = ctx.enter_context(tc.tile_pool(name="late_grouped", bufs=2))
        acc_pool = ctx.enter_context(tc.psum_pool(name="acc", bufs=1))
        flip_pool = ctx.enter_context(tc.psum_pool(name="flip", bufs=8 - LAST))

        ident = const.tile([P, P], F32, name="ident", align_bytes=ALIGN)
        b_rows = const.tile([P, P], BF16, name="b_rows")
        b_rows32 = const.tile([P, P], F32, name="b_rows32")
        one = const.tile([P, 1], F32, name="one")
        warm = const.tile([P, 2], F32, name="warm")
        differs = const.tile([P, VECTOR_TESTS, WORDS_PASS], F32, name="differs")
        distance = const.tile([P, n_chunks], F32, name="distance")
        distance_all = const.tile([P, 1], F32, name="distance_all")
        valid_col = const.tile([P, ROW_TILES], BF16, name="valid_col")
        ident16 = const.tile([P, P], BF16, name="ident16")
        in_sample = const.tile([P, P // TOKENS], BF16, name="in_sample")
        bias_col = const.tile([P, ROW_TILES], F32, name="bias_col")
        acc = [acc_pool.tile([P, ROWS], F32, name="acc%d" % m) for m in range(LAST)]

        last_banks = {}
        x_codes = []
        early_codes = []
        late_codes = []

        def multiply(r, m, s0=0, s1=SAMPLES):
            if m < SWEEP_TILES:
                (w_codes, w_scales), w0 = early_codes[r], P * m
            else:
                (w_codes, w_scales), w0 = late_codes[r // 2], P * (LATE_TILES * (r % 2) + m - SWEEP_TILES)
            w_cols = slice(w0, w0 + P)
            tokens = slice(TOKENS * s0, TOKENS * s1)
            nc.tensor.matmul_mx(
                out=last_banks[s0][:] if m == LAST else acc[m][:],
                lhsT=w_codes[:, w_cols].bitcast(FP8X4),
                lhsT_scale=w_scales[:, w_cols],
                rhs=x_codes[r][0][:, tokens].bitcast(FP8X4),
                rhs_scale=x_codes[r][1][:, tokens],
                start=(r == 0),
                stop=(r == ROUNDS - 1),
            )

        x_words = {}
        w_words = {}
        late_words = {}

        def words_of(nat):
            return nat[:].rearrange("p a k -> p (a k)").bitcast(F32)

        def load_chunk(c, w_natural):
            k0, width = K_PASS * first_round[c], K_PASS * CHUNK_ROUNDS[c]
            x_nat = natural.tile(
                [P, ROW_TILES, width], BF16, name="x_nat", tag="nat", align_bytes=ALIGN
            )
            w_nat = w_natural.tile(
                [P, SWEEP_TILES, width], BF16, name="w_nat", align_bytes=ALIGN
            )
            step = ROW_TILES // 2 if c == 0 else ROW_TILES
            for nat, rows, tiles in ((x_nat, x_rows, ROW_TILES), (w_nat, w_rows, SWEEP_TILES)):
                for a in range(0, tiles, step):
                    a1 = min(a + step, tiles)
                    nc.sync.dma_start(out=nat[:, a:a1, :], in_=rows[:, a:a1, k0 : k0 + width])
            x_words[c] = words_of(x_nat).rearrange("p (a w) -> p a w", a=ROW_TILES)
            w_words[c] = words_of(w_nat).rearrange("p (a w) -> p a w", a=SWEEP_TILES)

        def load_unit(g):
            k0, width = K_PASS * UNIT * g, K_PASS * UNIT
            nat = natural.tile(
                [P, LATE_TILES, width], BF16, name="late_nat", tag="nat", align_bytes=ALIGN
            )
            nc.sync.dma_start(out=nat[:], in_=w_rows[:, SWEEP_TILES:, k0 : k0 + width])
            late_words[g] = words_of(nat)

        loads = []
        for c in range(n_chunks):
            loads.append(c)
            if c in SORT_BEHIND_CHUNK:
                loads.append(n_chunks + SORT_BEHIND_CHUNK.index(c))
        loads += [n_chunks + g for g in range(len(SORT_BEHIND_CHUNK), UNITS)]

        def load_item(i, w_natural):
            if loads[i] < n_chunks:
                load_chunk(loads[i], w_natural)
            else:
                load_unit(loads[i] - n_chunks)

        def used_up(item, w_natural=None):
            i = loads.index(item) + LOADS_AHEAD
            if i < len(loads):
                load_item(i, w_natural)

        def flip_rows(columns):
            bank = flip_pool.tile([P, 2, 2, P], F32, name="flip")
            for i in range(2):
                for u in range(2):
                    nc.tensor.transpose(bank[:, i, u, :], columns(i, u), ident[:])
            return bank

        def gather_words(bank, rows4):
            nc.scalar.copy(
                out=rows4.bitcast(F32).rearrange("p (i r u) -> p i r u", i=2, u=2),
                in_=bank[:].rearrange("p i u r -> p i r u"),
            )

        def quantise(rows4, n_rows, bufs, label):
            codes = packed.tile([P, n_rows], U32, name="%s_codes" % label, align_bytes=ALIGN, bufs=bufs)
            scales = packed.tile([P, n_rows], U8, name="%s_scales" % label, align_bytes=ALIGN, bufs=bufs)
            nc.vector.quantize_mx(out=codes[:].bitcast(FP8X4), scales=scales[:], in_=rows4)
            return codes, scales

        late_sorted = {}

        def sort_words(g):
            tile_g = sorted_pool.tile(
                [P, LATE_TILES * UNIT * K_PASS], BF16, name="late_sorted", align_bytes=ALIGN
            )
            flat = tile_g[:].bitcast(F32)
            nc.vector.tensor_copy(
                out=flat.rearrange("p (j u q) -> p j u q", u=2, q=P),
                in_=late_words[g].rearrange("p (j q u) -> p j u q", u=2, q=P),
            )
            late_sorted[g] = flat.rearrange("p (i j u q) -> p i j u q", i=LATE_TILES, u=2, q=P)

        with ExitStack() as sweep:
            w_natural = sweep.enter_context(tc.tile_pool(name="w_natural", bufs=3))
            grouped = sweep.enter_context(tc.tile_pool(name="grouped", bufs=3))

            for i in range(LOADS_AHEAD):
                load_item(i, w_natural)

            make_identity(nc, ident[:])
            nc.vector.memset(one[:], 1.0)
            nc.scalar.activation(out=warm[:, 0:1], in_=one[:], func=ACT.Gelu)
            nc.vector.memset(differs[:], 0.0)
            nc.vector.memset(b_rows[:], 0.0)
            nc.scalar.dma_start(out=b_rows[0:ROW_TILES, :], in_=b.rearrange("(m o) -> m o", o=P))

            def measure_distance(c):
                spare = grouped.tile([P, WORDS_PASS * CHUNK_ROUNDS[c]], BF16, name="spare", bufs=1)
                nc.scalar.activation(
                    out=spare[:],
                    in_=x_words[c][:, VECTOR_TESTS, :],
                    func=ACT.Abs,
                    bias=-PAD_WORD,
                    accum_out=distance[:, c : c + 1],
                )

            filled = 0
            multiplied = 0
            r = 0
            for c in range(n_chunks):
                for j in range(CHUNK_ROUNDS[c]):
                    w0, w1 = WORDS_PASS * j, WORDS_PASS * (j + 1)
                    if r == SETTLED_ROUND:
                        nc.vector.tensor_copy(out=b_rows32[:], in_=b_rows[:])
                        nc.vector.tensor_copy(out=ident16[:], in_=ident[:])
                        nc.vector.tensor_reduce(
                            out=in_sample[:],
                            in_=ident[:].rearrange("p (s t) -> p s t", t=TOKENS),
                            axis=AX.X,
                            op=ALU.max,
                        )
                    nc.vector.scalar_tensor_tensor(
                        out=differs[:],
                        in0=x_words[c][:, 0:VECTOR_TESTS, w0:w1],
                        scalar=PAD_WORD,
                        in1=differs[:],
                        op0=ALU.not_equal,
                        op1=ALU.max,
                    )
                    x_rows4 = grouped.tile([P, 4 * ROWS], BF16, name="x_rows4", align_bytes=ALIGN)
                    w_rows4 = grouped.tile([P, 8 * P], BF16, name="w_rows4", align_bytes=ALIGN)
                    for words, a, rows4 in (
                        (x_words[c], 0, x_rows4[:, : 8 * P]),
                        (x_words[c], 2, x_rows4[:, 8 * P :]),
                        (w_words[c], 0, w_rows4[:]),
                    ):
                        bank = flip_rows(lambda i, u: words[:, a + i, w0 + u : w1 : 2])
                        gather_words(bank, rows4)
                        filled += 1
                        if filled % RUN_BANKS == 0:
                            while multiplied <= r - PASS_LAG:
                                for m in range(SWEEP_TILES):
                                    multiply(multiplied, m)
                                multiplied += 1
                    if j == 0:
                        measure_distance(c)
                    if r == ROUNDS - 1:
                        nc.vector.tensor_reduce(
                            out=valid_col[:, 0:VECTOR_TESTS], in_=differs[:], axis=AX.X, op=ALU.max
                        )
                        nc.vector.tensor_reduce(
                            out=distance_all[:], in_=distance[:], axis=AX.X, op=ALU.max
                        )
                        nc.vector.tensor_single_scalar(
                            out=valid_col[:, VECTOR_TESTS:], in_=distance_all[:], scalar=0.0, op=ALU.is_gt
                        )
                    x_codes.append(quantise(x_rows4[:], ROWS, ROUNDS, "x"))
                    early_codes.append(quantise(w_rows4[:], SWEEP_TILES * P, PASS_LAG + 2, "w_early"))
                    r += 1
                used_up(c, w_natural)
                if c in SORT_BEHIND_CHUNK:
                    g = SORT_BEHIND_CHUNK.index(c)
                    sort_words(g)
                    used_up(n_chunks + g, w_natural)

        tail = ctx.enter_context(tc.tile_pool(name="tail", bufs=2))
        units = [(m, 0, SAMPLES) for m in range(LAST)]
        for g in range(len(LAST_GROUPS)):
            units.append((LAST, sum(LAST_GROUPS[:g]), sum(LAST_GROUPS[: g + 1])))
        stats = const.tile([P, SAMPLES, 2, ROW_TILES], F32, name="stats")
        variance = const.tile([P, SAMPLES, ROW_TILES], F32, name="variance")
        weight = tail.tile([P, 2, SAMPLES, TOKENS], F32, name="weight", bufs=1)
        y = {}
        share = {}
        away = {}
        squares = {}
        square_share = {}
        banks = {}

        def spread_flags():
            banks["small"] = flip_pool.tile([P, P + SAMPLES], F32, name="small", tag="flip")
            banks["valid"] = flip_pool.tile([P, ROWS], F32, name="valid", tag="flip")
            nc.tensor.transpose(banks["small"][:, 0:P], b_rows32[:], ident[:])
            per_tile = P // TOKENS
            for a in range(ROW_TILES):
                flags = valid_col[:, a : a + 1].to_broadcast([P, P])
                for o_cols, rhs in (
                    (banks["valid"][:, P * a : P * (a + 1)], ident16),
                    (banks["small"][:, P + per_tile * a : P + per_tile * (a + 1)], in_sample),
                ):
                    nc.tensor.matmul(out=o_cols, lhsT=flags, rhs=rhs[:], start=True, stop=True)

        def find_bias():
            nc.scalar.copy(out=bias_col[:], in_=banks["small"][:, 0:ROW_TILES])

        def find_weights():
            count = banks["small"][:, P : P + SAMPLES]
            n_floor = const.tile([P, 2, SAMPLES], F32, name="n_floor")
            nc.vector.tensor_scalar_max(out=n_floor[:, 0, :], in0=count, scalar1=1.0)
            nc.vector.tensor_scalar(
                out=n_floor[:, 1, :], in0=count, scalar1=-1.0, scalar2=1.0, op0=ALU.add, op1=ALU.max
            )
            n_inverse = const.tile([P, 2, SAMPLES], F32, name="n_inverse")
            nc.vector.reciprocal(out=n_inverse[:], in_=n_floor[:])
            for g in range(2):
                nc.vector.tensor_tensor(
                    out=weight[:, g],
                    in0=banks["valid"][:].rearrange("p (s t) -> p s t", t=TOKENS),
                    in1=n_inverse[:, g, :].unsqueeze(2).to_broadcast([P, SAMPLES, TOKENS]),
                    op=ALU.mult,
                )

        def gelu(i):
            m, s0, s1 = units[i]
            y[i] = tail.tile([P, s1 - s0, TOKENS], F32, name="y", bufs=len(units))
            nc.scalar.activation(
                out=y[i][:].rearrange("p s t -> p (s t)"),
                in_=last_banks[s0][:] if m == LAST else acc[m][:],
                func=ACT.Gelu,
                bias=bias_col[:, m : m + 1],
            )

        def find_share(i):
            share[i] = tail.tile([P, SAMPLES, TOKENS], F32, name="share")
            nc.vector.tensor_tensor(out=share[i][:], in0=y[i][:], in1=weight[:, 0], op=ALU.mult)

        def find_mean(i):
            nc.vector.tensor_reduce(out=stats[:, :, 1, i], in_=share[i][:], axis=AX.X, op=ALU.add)

        def find_away(i):
            shape = [P, SAMPLES, TOKENS]
            away[i] = tail.tile(shape, F32, name="away")
            nc.vector.tensor_tensor(
                out=away[i][:],
                in0=y[i][:],
                in1=stats[:, :, 1, i].unsqueeze(2).to_broadcast(shape),
                op=ALU.subtract,
            )

        def square(i):
            squares[i] = tail.tile([P, SAMPLES, TOKENS], F32, name="squares")
            nc.scalar.activation(out=squares[i][:], in_=away[i][:], func=ACT.Square)

        def find_square_share(i):
            square_share[i] = tail.tile([P, SAMPLES, TOKENS], F32, name="square_share", tag="share")
            nc.vector.tensor_tensor(
                out=square_share[i][:], in0=squares[i][:], in1=weight[:, 1], op=ALU.mult
            )

        def find_variance(i):
            nc.vector.tensor_reduce(
                out=variance[:, :, i], in_=square_share[i][:], axis=AX.X, op=ALU.add
            )

        beside = [
            [find_bias],
            [find_weights, lambda: gelu(0), lambda: gelu(1)],
            [],
            [],
            [lambda: find_share(0), lambda: find_share(1)],
            [],
            [lambda: find_mean(0), lambda: find_mean(1)],
            [lambda: find_away(0), lambda: find_away(1)],
        ]

        for g in range(UNITS):
            for pair in range(UNIT // 2):
                rows4 = late_grouped.tile([P, 16 * P], BF16, name="late_rows4", align_bytes=ALIGN)
                for j in range(2 * pair, 2 * pair + 2):
                    bank = flip_rows(lambda i, u: late_sorted[g][:, i, j, u, :])
                    gather_words(bank, rows4[:, 8 * P * (j % 2) : 8 * P * (j % 2 + 1)])
                late_codes.append(quantise(rows4[:], 4 * P, ROUNDS // 2, "w_late"))
            if g == 0:
                spread_flags()
                for r in range(multiplied, ROUNDS):
                    for m in range(SWEEP_TILES):
                        multiply(r, m)
            for r in range(UNIT * max(g - 1, 0), UNIT * g):
                multiply(r, SWEEP_TILES)
            if g in SORT_BEHIND_UNIT:
                later = len(SORT_BEHIND_CHUNK) + SORT_BEHIND_UNIT.index(g)
                sort_words(later)
                used_up(n_chunks + later)
            for step in beside[g]:
                step()

        for i in range(LAST, len(units)):
            m, s0, s1 = units[i]
            last_banks[s0] = acc_pool.tile(
                [P, TOKENS * (s1 - s0)], F32, name="last%d" % s0, tag="acc%d" % (i - LAST)
            )
        for r in range(FILL_PASSES):
            multiply(r, *units[LAST])
        for r in range(ROUNDS - UNIT, ROUNDS):
            multiply(r, SWEEP_TILES)
        for r in range(FILL_PASSES, ROUNDS):
            multiply(r, *units[LAST])
        for unit in units[LAST + 1 :]:
            for r in range(ROUNDS):
                multiply(r, *unit)

        for i in range(SWEEP_TILES):
            square(i)
        for i in range(SWEEP_TILES):
            find_square_share(i)
        for i in range(SWEEP_TILES):
            find_variance(i)
        gelu(SWEEP_TILES)
        find_share(SWEEP_TILES)
        find_mean(SWEEP_TILES)
        find_away(SWEEP_TILES)
        square(SWEEP_TILES)
        gelu(LAST)
        find_square_share(SWEEP_TILES)
        find_variance(SWEEP_TILES)

        for i in range(LAST, len(units)):
            m, s0, s1 = units[i]
            if i + 1 < len(units):
                gelu(i + 1)
            spare = tail.tile([P, s1 - s0, TOKENS], F32, name="spare")
            away_share = tail.tile([P, s1 - s0, TOKENS], F32, name="away_share")
            for s in range(s0, s1):
                nc.vector.scalar_tensor_tensor(
                    out=spare[:, s - s0, :],
                    in0=y[i][:, s - s0, :],
                    scalar=1.0,
                    in1=weight[:, 0, s, :],
                    op0=ALU.mult,
                    op1=ALU.mult,
                    accum_out=stats[:, s : s + 1, 1, m],
                )
            for s in range(s0, s1):
                nc.vector.scalar_tensor_tensor(
                    out=away_share[:, s - s0, :],
                    in0=y[i][:, s - s0, :],
                    scalar=stats[:, s : s + 1, 1, m],
                    in1=weight[:, 1, s, :],
                    op0=ALU.subtract,
                    op1=ALU.mult,
                )
            for s in range(s0, s1):
                nc.vector.scalar_tensor_tensor(
                    out=spare[:, s - s0, :],
                    in0=y[i][:, s - s0, :],
                    scalar=stats[:, s : s + 1, 1, m],
                    in1=away_share[:, s - s0, :],
                    op0=ALU.subtract,
                    op1=ALU.mult,
                    accum_out=variance[:, s : s + 1, m],
                )
        nc.scalar.activation(out=warm[:, 1:2], in_=one[:], func=ACT.Sqrt)

        root = const.tile([P, SAMPLES, ROW_TILES], F32, name="root")
        nc.scalar.activation(out=root[:], in_=variance[:], func=ACT.Sqrt, bias=SQRT_FLOOR)
        some = const.tile([P, SAMPLES, ROW_TILES], F32, name="some")
        nc.vector.tensor_single_scalar(out=some[:], in_=variance[:], scalar=0.0, op=ALU.is_gt)
        nc.vector.tensor_tensor(out=stats[:, :, 0, :], in0=root[:], in1=some[:], op=ALU.mult)

        stats_bank = flip_pool.tile([P, P], F32, name="stats_bank", tag="flip")
        nc.tensor.transpose(stats_bank[:], stats[:].rearrange("p s g m -> p (s g m)"), ident[:])
        result = const.tile([P, P], F32, name="result")
        nc.vector.tensor_copy(out=result[:], in_=stats_bank[:])
        nc.sync.dma_start(out=out.rearrange("s (g o) -> (s g) o", o=P), in_=result[:])
